import numpy as np
import ml_dtypes


def mxq(x, axis, fmt="e4m3"):
    dtype, down = {"e4m3": (ml_dtypes.float8_e4m3fn, 7), "e5m2": (ml_dtypes.float8_e5m2, 14)}[fmt]
    v = np.moveaxis(np.asarray(x, np.float32).astype(ml_dtypes.bfloat16).astype(np.float64), axis, -1)
    blocks = v.reshape(v.shape[:-1] + (-1, 32))
    amax = np.abs(blocks).max(-1, keepdims=True)
    byte = np.maximum(np.where(amax > 0, np.frexp(amax)[1] - 1 + 127, 0) - down, 1)
    scale = np.exp2(byte - 127.0)
    codes = (blocks / scale).astype(np.float32).astype(dtype).astype(np.float64)
    return np.moveaxis((codes * scale).reshape(v.shape), -1, axis)


WIDE = False


def mx_kscale(k):
    if not WIDE:
        return np.ones(k)
    levels = np.array([10, -10, 5, -5, 0])
    a = np.random.permutation(np.resize(levels, k // 512 * 4)).reshape(k // 512, 4)
    idx = np.arange(k)
    return np.exp2(a[idx // 512, idx % 128 // 32])


BF16 = ml_dtypes.bfloat16


def bf(x):
    return np.asarray(x, np.float32).astype(BF16)


def f64(x):
    return np.asarray(x).astype(np.float64)


SQ, B, H, NP, HN, MQG = 4096, 2, 1024, 2, 64, 1
ROT = HN // 2
QD, KVD = NP * HN, MQG * HN
QKV = QD + 2 * KVD
ROPE_BASE = 10000.0


def apply_rope(x, rope):
    sq, b, nh, hn = x.shape
    rot = rope.shape[-2] * 2
    xr, xp = x[..., :rot], x[..., rot:]
    xs = xr.reshape(sq, b, nh, rot // 2, 2)
    rc = rope[:sq].reshape(sq, -1, 1, rot // 2, 2)
    o0 = xs[..., 0] * rc[..., 0] - xs[..., 1] * rc[..., 1]
    o1 = xs[..., 1] * rc[..., 0] + xs[..., 0] * rc[..., 1]
    rotated = np.stack([o0, o1], -1).reshape(sq, b, nh, rot)
    return np.concatenate([rotated, xp], axis=-1)


def setup_inputs():
    s = mx_kscale(H)
    pos = np.arange(SQ, dtype=np.float64)
    inv = 1.0 / (ROPE_BASE ** (np.arange(0, ROT, 2, dtype=np.float64) / ROT))
    ang = pos[:, None] * inv[None, :]
    rope = np.stack([np.cos(ang), np.sin(ang)], -1)[:, None, :, :]
    return {"hidden_states": bf(np.random.standard_normal((SQ, B, H)) * s),
            "Wqkv": bf(np.random.standard_normal((QKV, H)) * 1.3 / np.sqrt(H) / s[None, :]),
            "bqkv": bf(np.random.standard_normal(QKV) * 0.3),
            "rotary_pos_emb": bf(rope)}


def reference(hidden_states, Wqkv, bqkv, rotary_pos_emb):
    x = f64(hidden_states)
    rope = f64(rotary_pos_emb)
    sq, b, _ = x.shape
    mixed = (mxq(x, 2, "e4m3") @ mxq(f64(Wqkv), 1, "e4m3").T) + f64(bqkv)
    q = mixed[..., :QD].reshape(sq, b, NP, HN)
    k = mixed[..., QD:QD + KVD].reshape(sq, b, MQG, HN)
    v = mixed[..., QD + KVD:].reshape(sq, b, MQG, HN)
    return apply_rope(q, rope), apply_rope(k, rope), v

@@ -1,0 +1,217 @@
+from contextlib import ExitStack
+
+import concourse.mybir as mybir
+from concourse.masks import make_identity
+
+F32 = mybir.dt.float32
+BF16 = mybir.dt.bfloat16
+U32 = mybir.dt.uint32
+U8 = mybir.dt.uint8
+FP8X4 = mybir.dt.float8_e4m3fn_x4
+ADD = mybir.AluOpType.add
+MULT = mybir.AluOpType.mult
+
+P = 128
+POSITIONS, BATCH, WIDTH = 4096, 2, 1024
+Q_COLS, K_COLS, V_COLS = 128, 64, 64
+FEATURES = Q_COLS + K_COLS + V_COLS
+HEAD = 64
+ROTATED = 32
+PAIRS = ROTATED // 2
+
+PACK = 4
+PASSES = WIDTH // (P * PACK)
+HALVES = 2
+
+TILES = POSITIONS * BATCH // P
+ROUND = 4
+ROUNDS = TILES // ROUND
+ROUND_POSITIONS = ROUND // BATCH
+LOOKAHEAD = 5
+
+FLOPS = 2 * POSITIONS * BATCH * WIDTH * FEATURES
+
+
+def k_onto_partitions(nc, banks, identity, rows_words, grouped_words):
+    bank = banks.tile([P, PASSES, HALVES, P], F32, tag="turned")
+    for g in range(PASSES):
+        for u in range(HALVES):
+            first = (g * HALVES + u) * P
+            nc.tensor.transpose(bank[:, g, u, :], rows_words[:, first : first + P], identity)
+    nc.scalar.copy(out=grouped_words, in_=bank[:].rearrange("p g u r -> p g r u"))
+
+
+def rotate(nc, scratch, heads, cos_sin, minus_sin_cos):
+    shape = [P, heads.shape[1], heads.shape[2], PAIRS, 2]
+    rotated = heads[:, :, :, 0:ROTATED].rearrange("p i m (j e) -> p i m j e", e=2)
+    from_even = scratch.tile(shape, F32, tag="from_even%d" % shape[2])
+    from_odd = scratch.tile(shape, F32, tag="from_odd%d" % shape[2])
+    nc.vector.tensor_tensor(
+        out=from_even[:],
+        in0=rotated[:, :, :, :, 0:1].to_broadcast(shape),
+        in1=cos_sin.unsqueeze(2).to_broadcast(shape),
+        op=MULT,
+    )
+    nc.vector.tensor_tensor(
+        out=from_odd[:],
+        in0=rotated[:, :, :, :, 1:2].to_broadcast(shape),
+        in1=minus_sin_cos.unsqueeze(2).to_broadcast(shape),
+        op=MULT,
+    )
+    return rotated, from_even, from_odd
+
+
+def tile_selfattention_pa_t_kernel(
+    tc, hidden_states, Wqkv, bqkv, rotary_pos_emb, out_0, out_1, out_2
+):
+    nc = tc.nc
+    per_partition = POSITIONS // P
+    x_dram = hidden_states.rearrange("(p s) b h -> p (s b) h", s=per_partition)
+    q_dram = out_0.rearrange("(p s) b n d -> p (s b) (n d)", s=per_partition)
+    k_dram = out_1.rearrange("(p s) b n d -> p (s b) (n d)", s=per_partition)
+    v_dram = out_2.rearrange("(p s) b n d -> p (s b) (n d)", s=per_partition)
+    rope_dram = rotary_pos_emb.rearrange("(p s) o j c -> p s (o j) c", s=per_partition)
+
+    with ExitStack() as ctx:
+        ctx.enter_context(tc.manual_schedule())
+        const = ctx.enter_context(tc.tile_pool(name="const", bufs=1))
+        x_pool = ctx.enter_context(tc.tile_pool(name="x", bufs=LOOKAHEAD + 1))
+        mx_pool = ctx.enter_context(tc.tile_pool(name="mx", bufs=3))
+        out_pool = ctx.enter_context(tc.tile_pool(name="out", bufs=3))
+        scratch = ctx.enter_context(tc.tile_pool(name="scratch", bufs=2))
+        turned_banks = ctx.enter_context(tc.psum_pool(name="turned", bufs=4))
+        acc_banks = ctx.enter_context(tc.psum_pool(name="acc", bufs=4))
+
+        w_rows = const.tile([P, FEATURES // P, WIDTH], BF16)
+        nc.sync.dma_start(out=w_rows[:], in_=Wqkv.rearrange("(i p) k -> p i k", p=P))
+        x_rounds = {}
+
+        def load_round(r):
+            x_rows = x_pool.tile([P, ROUND, WIDTH], BF16)
+            nc.sync.dma_start(out=x_rows[:], in_=x_dram[:, r * ROUND : (r + 1) * ROUND, :])
+            x_rounds[r] = x_rows
+
+        for r in range(LOOKAHEAD):
+            load_round(r)
+
+        rope_rows = const.tile([P, per_partition, PAIRS, 2], BF16)
+        nc.scalar.dma_start(out=rope_rows[:], in_=rope_dram)
+        bias = const.tile([P, FEATURES], BF16)
+        nc.scalar.dma_start(out=bias[:], in_=bqkv.partition_broadcast(P))
+
+        identity = const.tile([P, P], F32)
+        make_identity(nc, identity[:])
+
+        cos_sin = const.tile([P, per_partition, PAIRS, 2], F32)
+        minus_sin_cos = const.tile([P, per_partition, PAIRS, 2], F32)
+        nc.vector.tensor_copy(out=cos_sin[:], in_=rope_rows[:])
+        nc.vector.tensor_scalar_mul(
+            out=minus_sin_cos[:, :, :, 0:1], in0=rope_rows[:, :, :, 1:2], scalar1=-1.0
+        )
+        nc.vector.tensor_copy(out=minus_sin_cos[:, :, :, 1:2], in_=rope_rows[:, :, :, 0:1])
+
+        w_grouped = const.tile([P, PASSES, FEATURES, PACK], BF16, align_bytes=64)
+        w_codes = const.tile([P, PASSES, FEATURES], U32, align_bytes=64)
+        w_scales = const.tile([P, PASSES, FEATURES], U8, align_bytes=64)
+        for i in range(FEATURES // P):
+            k_onto_partitions(
+                nc,
+                turned_banks,
+                identity[:],
+                w_rows[:, i, :].bitcast(F32),
+                w_grouped[:].bitcast(F32)[:, :, i * P : (i + 1) * P, :],
+            )
+        nc.vector.quantize_mx(
+            out=w_codes[:].rearrange("p g n -> p (g n)").bitcast(FP8X4),
+            scales=w_scales[:].rearrange("p g n -> p (g n)"),
+            in_=w_grouped[:].rearrange("p g n k -> p (g n k)"),
+        )
+
+        grouped_rounds, codes_rounds, acc_rounds = {}, {}, {}
+
+        def turn_round(r):
+            x_grouped = mx_pool.tile([P, ROUND, PASSES, P, PACK], BF16, align_bytes=64)
+            for t in range(ROUND):
+                k_onto_partitions(
+                    nc,
+                    turned_banks,
+                    identity[:],
+                    x_rounds[r][:, t, :].bitcast(F32),
+                    x_grouped[:, t].bitcast(F32),
+                )
+            grouped_rounds[r] = x_grouped
+
+        def quantise_round(r):
+            x_codes = mx_pool.tile([P, ROUND, PASSES, P], U32, align_bytes=64)
+            x_scales = mx_pool.tile([P, ROUND, PASSES, P], U8, align_bytes=64)
+            nc.vector.quantize_mx(
+                out=x_codes[:].rearrange("p t g r -> p (t g r)").bitcast(FP8X4),
+                scales=x_scales[:].rearrange("p t g r -> p (t g r)"),
+                in_=grouped_rounds[r][:].rearrange("p t g r k -> p (t g r k)"),
+            )
+            codes_rounds[r] = (x_codes, x_scales)
+
+        def multiply_round(r):
+            x_codes, x_scales = codes_rounds[r]
+            acc_rounds[r] = []
+            for i in range(ROUND_POSITIONS):
+                acc = acc_banks.tile([P, BATCH, FEATURES], F32)
+                for b in range(BATCH):
+                    for g in range(PASSES):
+                        nc.tensor.matmul_mx(
+                            out=acc[:, b, :],
+                            lhsT=x_codes[:, i * BATCH + b, g, :].bitcast(FP8X4),
+                            lhsT_scale=x_scales[:, i * BATCH + b, g, :],
+                            rhs=w_codes[:, g, :].bitcast(FP8X4),
+                            rhs_scale=w_scales[:, g, :],
+                            start=(g == 0),
+                            stop=(g == PASSES - 1),
+                        )
+                acc_rounds[r].append(acc)
+
+        def finish_round(r):
+            q_rows = out_pool.tile([P, ROUND, Q_COLS], F32)
+            k_rows = out_pool.tile([P, ROUND, K_COLS], F32)
+            v_rows = out_pool.tile([P, ROUND, V_COLS], F32)
+            parts = ((q_rows, 0, Q_COLS), (k_rows, Q_COLS, K_COLS), (v_rows, Q_COLS + K_COLS, V_COLS))
+            for i in range(ROUND_POSITIONS):
+                acc = acc_rounds[r][i]
+                for rows, first, cols in parts:
+                    nc.vector.tensor_tensor(
+                        out=rows[:, i * BATCH : (i + 1) * BATCH, :],
+                        in0=acc[:, :, first : first + cols],
+                        in1=bias[:, first : first + cols].unsqueeze(1).to_broadcast([P, BATCH, cols]),
+                        op=ADD,
+                    )
+            positions = slice(r * ROUND_POSITIONS, (r + 1) * ROUND_POSITIONS)
+            q_terms = rotate(
+                nc,
+                scratch,
+                q_rows[:].rearrange("p (i b) (n d) -> p i (b n) d", b=BATCH, d=HEAD),
+                cos_sin[:, positions],
+                minus_sin_cos[:, positions],
+            )
+            k_terms = rotate(
+                nc,
+                scratch,
+                k_rows[:].rearrange("p (i b) d -> p i b d", b=BATCH),
+                cos_sin[:, positions],
+                minus_sin_cos[:, positions],
+            )
+            for rotated, from_even, from_odd in (q_terms, k_terms):
+                nc.vector.tensor_tensor(out=rotated, in0=from_even[:], in1=from_odd[:], op=ADD)
+            tiles = slice(r * ROUND, (r + 1) * ROUND)
+            nc.sync.dma_start(out=q_dram[:, tiles, :], in_=q_rows[:])
+            nc.sync.dma_start(out=k_dram[:, tiles, :], in_=k_rows[:])
+            nc.sync.dma_start(out=v_dram[:, tiles, :], in_=v_rows[:])
+
+        for n in range(ROUNDS + 2):
+            if n + LOOKAHEAD < ROUNDS:
+                load_round(n + LOOKAHEAD)
+            if n < ROUNDS:
+                turn_round(n)
+            if 1 <= n <= ROUNDS:
+                quantise_round(n - 1)
+                multiply_round(n - 1)
+            if n >= 2:
+                finish_round(n - 2)

@@ -23,11 +23,9 @@ PACK = 4
 PASSES = WIDTH // (P * PACK)
 HALVES = 2
 
-TILES = POSITIONS * BATCH // P
-ROUND = 4
-ROUNDS = TILES // ROUND
-ROUND_POSITIONS = ROUND // BATCH
-LOOKAHEAD = 5
+STEPS = POSITIONS // P
+BLOCK = 2
+LOOKAHEAD = 8
 
 FLOPS = 2 * POSITIONS * BATCH * WIDTH * FEATURES
 
@@ -41,7 +39,7 @@ def k_onto_partitions(nc, banks, identity, rows_words, grouped_words):
     nc.scalar.copy(out=grouped_words, in_=bank[:].rearrange("p g u r -> p g r u"))
 
 
-def rotate(nc, scratch, heads, cos_sin, minus_sin_cos):
+def rotation_terms(nc, scratch, heads, cos_sin, minus_sin_cos):
     shape = [P, heads.shape[1], heads.shape[2], PAIRS, 2]
     rotated = heads[:, :, :, 0:ROTATED].rearrange("p i m (j e) -> p i m j e", e=2)
     from_even = scratch.tile(shape, F32, tag="from_even%d" % shape[2])
@@ -65,12 +63,11 @@ def tile_selfattention_pa_t_kernel(
     tc, hidden_states, Wqkv, bqkv, rotary_pos_emb, out_0, out_1, out_2
 ):
     nc = tc.nc
-    per_partition = POSITIONS // P
-    x_dram = hidden_states.rearrange("(p s) b h -> p (s b) h", s=per_partition)
-    q_dram = out_0.rearrange("(p s) b n d -> p (s b) (n d)", s=per_partition)
-    k_dram = out_1.rearrange("(p s) b n d -> p (s b) (n d)", s=per_partition)
-    v_dram = out_2.rearrange("(p s) b n d -> p (s b) (n d)", s=per_partition)
-    rope_dram = rotary_pos_emb.rearrange("(p s) o j c -> p s (o j) c", s=per_partition)
+    x_dram = hidden_states.rearrange("(p s) b h -> p s b h", s=STEPS)
+    q_dram = out_0.rearrange("(p s) b n d -> p s (b n d)", s=STEPS)
+    k_dram = out_1.rearrange("(p s) b n d -> p s (b n d)", s=STEPS)
+    v_dram = out_2.rearrange("(p s) b n d -> p s (b n d)", s=STEPS)
+    rope_dram = rotary_pos_emb.rearrange("(p s) o j c -> p s (o j) c", s=STEPS)
 
     with ExitStack() as ctx:
         ctx.enter_context(tc.manual_schedule())
@@ -84,17 +81,17 @@ def tile_selfattention_pa_t_kernel(
 
         w_rows = const.tile([P, FEATURES // P, WIDTH], BF16)
         nc.sync.dma_start(out=w_rows[:], in_=Wqkv.rearrange("(i p) k -> p i k", p=P))
-        x_rounds = {}
+        x_steps = {}
 
-        def load_round(r):
-            x_rows = x_pool.tile([P, ROUND, WIDTH], BF16)
-            nc.sync.dma_start(out=x_rows[:], in_=x_dram[:, r * ROUND : (r + 1) * ROUND, :])
-            x_rounds[r] = x_rows
+        def load_step(s):
+            x_rows = x_pool.tile([P, BATCH, WIDTH], BF16)
+            nc.sync.dma_start(out=x_rows[:], in_=x_dram[:, s])
+            x_steps[s] = x_rows
 
-        for r in range(LOOKAHEAD):
-            load_round(r)
+        for s in range(LOOKAHEAD):
+            load_step(s)
 
-        rope_rows = const.tile([P, per_partition, PAIRS, 2], BF16)
+        rope_rows = const.tile([P, STEPS, PAIRS, 2], BF16)
         nc.scalar.dma_start(out=rope_rows[:], in_=rope_dram)
         bias = const.tile([P, FEATURES], BF16)
         nc.scalar.dma_start(out=bias[:], in_=bqkv.partition_broadcast(P))
@@ -102,8 +99,8 @@ def tile_selfattention_pa_t_kernel(
         identity = const.tile([P, P], F32)
         make_identity(nc, identity[:])
 
-        cos_sin = const.tile([P, per_partition, PAIRS, 2], F32)
-        minus_sin_cos = const.tile([P, per_partition, PAIRS, 2], F32)
+        cos_sin = const.tile([P, STEPS, PAIRS, 2], F32)
+        minus_sin_cos = const.tile([P, STEPS, PAIRS, 2], F32)
         nc.vector.tensor_copy(out=cos_sin[:], in_=rope_rows[:])
         nc.vector.tensor_scalar_mul(
             out=minus_sin_cos[:, :, :, 0:1], in0=rope_rows[:, :, :, 1:2], scalar1=-1.0
@@ -127,91 +124,91 @@ def tile_selfattention_pa_t_kernel(
             in_=w_grouped[:].rearrange("p g n k -> p (g n k)"),
         )
 
-        grouped_rounds, codes_rounds, acc_rounds = {}, {}, {}
+        grouped_steps, codes_steps, acc_steps, out_blocks = {}, {}, {}, {}
 
-        def turn_round(r):
-            x_grouped = mx_pool.tile([P, ROUND, PASSES, P, PACK], BF16, align_bytes=64)
-            for t in range(ROUND):
+        def turn_step(s):
+            x_grouped = mx_pool.tile([P, BATCH, PASSES, P, PACK], BF16, align_bytes=64)
+            for b in range(BATCH):
                 k_onto_partitions(
                     nc,
                     turned_banks,
                     identity[:],
-                    x_rounds[r][:, t, :].bitcast(F32),
-                    x_grouped[:, t].bitcast(F32),
+                    x_steps[s][:, b, :].bitcast(F32),
+                    x_grouped[:, b].bitcast(F32),
                 )
-            grouped_rounds[r] = x_grouped
+            grouped_steps[s] = x_grouped
 
-        def quantise_round(r):
-            x_codes = mx_pool.tile([P, ROUND, PASSES, P], U32, align_bytes=64)
-            x_scales = mx_pool.tile([P, ROUND, PASSES, P], U8, align_bytes=64)
+        def quantise_step(s):
+            x_codes = mx_pool.tile([P, BATCH, PASSES, P], U32, align_bytes=64)
+            x_scales = mx_pool.tile([P, BATCH, PASSES, P], U8, align_bytes=64)
             nc.vector.quantize_mx(
-                out=x_codes[:].rearrange("p t g r -> p (t g r)").bitcast(FP8X4),
-                scales=x_scales[:].rearrange("p t g r -> p (t g r)"),
-                in_=grouped_rounds[r][:].rearrange("p t g r k -> p (t g r k)"),
+                out=x_codes[:].rearrange("p b g r -> p (b g r)").bitcast(FP8X4),
+                scales=x_scales[:].rearrange("p b g r -> p (b g r)"),
+                in_=grouped_steps[s][:].rearrange("p b g r k -> p (b g r k)"),
             )
-            codes_rounds[r] = (x_codes, x_scales)
+            codes_steps[s] = (x_codes, x_scales)
 
-        def multiply_round(r):
-            x_codes, x_scales = codes_rounds[r]
-            acc_rounds[r] = []
-            for i in range(ROUND_POSITIONS):
-                acc = acc_banks.tile([P, BATCH, FEATURES], F32)
-                for b in range(BATCH):
-                    for g in range(PASSES):
-                        nc.tensor.matmul_mx(
-                            out=acc[:, b, :],
-                            lhsT=x_codes[:, i * BATCH + b, g, :].bitcast(FP8X4),
-                            lhsT_scale=x_scales[:, i * BATCH + b, g, :],
-                            rhs=w_codes[:, g, :].bitcast(FP8X4),
-                            rhs_scale=w_scales[:, g, :],
-                            start=(g == 0),
-                            stop=(g == PASSES - 1),
-                        )
-                acc_rounds[r].append(acc)
-
-        def finish_round(r):
-            q_rows = out_pool.tile([P, ROUND, Q_COLS], F32)
-            k_rows = out_pool.tile([P, ROUND, K_COLS], F32)
-            v_rows = out_pool.tile([P, ROUND, V_COLS], F32)
-            parts = ((q_rows, 0, Q_COLS), (k_rows, Q_COLS, K_COLS), (v_rows, Q_COLS + K_COLS, V_COLS))
-            for i in range(ROUND_POSITIONS):
-                acc = acc_rounds[r][i]
-                for rows, first, cols in parts:
-                    nc.vector.tensor_tensor(
-                        out=rows[:, i * BATCH : (i + 1) * BATCH, :],
-                        in0=acc[:, :, first : first + cols],
-                        in1=bias[:, first : first + cols].unsqueeze(1).to_broadcast([P, BATCH, cols]),
-                        op=ADD,
+        def multiply_step(s):
+            x_codes, x_scales = codes_steps[s]
+            acc = acc_banks.tile([P, BATCH, FEATURES], F32)
+            for b in range(BATCH):
+                for g in range(PASSES):
+                    nc.tensor.matmul_mx(
+                        out=acc[:, b, :],
+                        lhsT=x_codes[:, b, g, :].bitcast(FP8X4),
+                        lhsT_scale=x_scales[:, b, g, :],
+                        rhs=w_codes[:, g, :].bitcast(FP8X4),
+                        rhs_scale=w_scales[:, g, :],
+                        start=(g == 0),
+                        stop=(g == PASSES - 1),
                     )
-            positions = slice(r * ROUND_POSITIONS, (r + 1) * ROUND_POSITIONS)
-            q_terms = rotate(
+            acc_steps[s] = acc
+
+        def add_bias_step(s):
+            if s % BLOCK == 0:
+                q_rows = out_pool.tile([P, BLOCK, BATCH, Q_COLS], F32)
+                k_rows = out_pool.tile([P, BLOCK, BATCH, K_COLS], F32)
+                v_rows = out_pool.tile([P, BLOCK, BATCH, V_COLS], F32)
+                out_blocks[s // BLOCK] = (q_rows, k_rows, v_rows)
+            first = 0
+            for rows in out_blocks[s // BLOCK]:
+                cols = rows.shape[3]
+                nc.vector.tensor_tensor(
+                    out=rows[:, s % BLOCK],
+                    in0=acc_steps[s][:, :, first : first + cols],
+                    in1=bias[:, first : first + cols].unsqueeze(1).to_broadcast([P, BATCH, cols]),
+                    op=ADD,
+                )
+                first += cols
+
+        def rotate_and_store_block(c):
+            q_rows, k_rows, v_rows = out_blocks[c]
+            steps = slice(c * BLOCK, (c + 1) * BLOCK)
+            nc.sync.dma_start(out=v_dram[:, steps], in_=v_rows[:].rearrange("p i b c -> p i (b c)"))
+            q_terms = rotation_terms(
                 nc,
                 scratch,
-                q_rows[:].rearrange("p (i b) (n d) -> p i (b n) d", b=BATCH, d=HEAD),
-                cos_sin[:, positions],
-                minus_sin_cos[:, positions],
+                q_rows[:].rearrange("p i b (n d) -> p i (b n) d", d=HEAD),
+                cos_sin[:, steps],
+                minus_sin_cos[:, steps],
             )
-            k_terms = rotate(
-                nc,
-                scratch,
-                k_rows[:].rearrange("p (i b) d -> p i b d", b=BATCH),
-                cos_sin[:, positions],
-                minus_sin_cos[:, positions],
+            k_terms = rotation_terms(
+                nc, scratch, k_rows[:], cos_sin[:, steps], minus_sin_cos[:, steps]
             )
             for rotated, from_even, from_odd in (q_terms, k_terms):
                 nc.vector.tensor_tensor(out=rotated, in0=from_even[:], in1=from_odd[:], op=ADD)
-            tiles = slice(r * ROUND, (r + 1) * ROUND)
-            nc.sync.dma_start(out=q_dram[:, tiles, :], in_=q_rows[:])
-            nc.sync.dma_start(out=k_dram[:, tiles, :], in_=k_rows[:])
-            nc.sync.dma_start(out=v_dram[:, tiles, :], in_=v_rows[:])
+            nc.sync.dma_start(out=q_dram[:, steps], in_=q_rows[:].rearrange("p i b c -> p i (b c)"))
+            nc.sync.dma_start(out=k_dram[:, steps], in_=k_rows[:].rearrange("p i b c -> p i (b c)"))
 
-        for n in range(ROUNDS + 2):
-            if n + LOOKAHEAD < ROUNDS:
-                load_round(n + LOOKAHEAD)
-            if n < ROUNDS:
-                turn_round(n)
-            if 1 <= n <= ROUNDS:
-                quantise_round(n - 1)
-                multiply_round(n - 1)
+        for n in range(STEPS + 2):
+            if n + LOOKAHEAD < STEPS:
+                load_step(n + LOOKAHEAD)
+            if n < STEPS:
+                turn_step(n)
+            if 1 <= n <= STEPS:
+                quantise_step(n - 1)
+                multiply_step(n - 1)
             if n >= 2:
-                finish_round(n - 2)
+                add_bias_step(n - 2)
+                if (n - 2) % BLOCK == BLOCK - 1:
+                    rotate_and_store_block((n - 2) // BLOCK)

@@ -77,7 +77,8 @@ def tile_selfattention_pa_t_kernel(
         out_pool = ctx.enter_context(tc.tile_pool(name="out", bufs=3))
         scratch = ctx.enter_context(tc.tile_pool(name="scratch", bufs=2))
         turned_banks = ctx.enter_context(tc.psum_pool(name="turned", bufs=4))
-        acc_banks = ctx.enter_context(tc.psum_pool(name="acc", bufs=4))
+        acc_banks = ctx.enter_context(tc.psum_pool(name="acc", bufs=3))
+        spare_banks = ctx.enter_context(tc.psum_pool(name="spare", bufs=1))
 
         w_rows = const.tile([P, FEATURES // P, WIDTH], BF16)
         nc.sync.dma_start(out=w_rows[:], in_=Wqkv.rearrange("(i p) k -> p i k", p=P))
@@ -125,6 +126,7 @@ def tile_selfattention_pa_t_kernel(
         )
 
         grouped_steps, codes_steps, acc_steps, out_blocks = {}, {}, {}, {}
+        unread = spare_banks.tile([P, PASSES * FEATURES], F32)
 
         def turn_step(s):
             x_grouped = mx_pool.tile([P, BATCH, PASSES, P, PACK], BF16, align_bytes=64)
@@ -163,6 +165,15 @@ def tile_selfattention_pa_t_kernel(
                         stop=(g == PASSES - 1),
                     )
             acc_steps[s] = acc
+            nc.tensor.matmul_mx(
+                out=unread[:],
+                lhsT=x_codes[:, 0, 0, :].bitcast(FP8X4),
+                lhsT_scale=x_scales[:, 0, 0, :],
+                rhs=w_codes[:].rearrange("p g n -> p (g n)").bitcast(FP8X4),
+                rhs_scale=w_scales[:].rearrange("p g n -> p (g n)"),
+                start=True,
+                stop=True,
+            )
 
         def add_bias_step(s):
             if s % BLOCK == 0:

@@ -13,9 +13,9 @@ MULT = mybir.AluOpType.mult
 
 P = 128
 POSITIONS, BATCH, WIDTH = 4096, 2, 1024
-Q_COLS, K_COLS, V_COLS = 128, 64, 64
-FEATURES = Q_COLS + K_COLS + V_COLS
 HEAD = 64
+FEATURES = 4 * HEAD
+HALF = 2 * HEAD
 ROTATED = 32
 PAIRS = ROTATED // 2
 
@@ -23,9 +23,11 @@ PACK = 4
 PASSES = WIDTH // (P * PACK)
 HALVES = 2
 
-STEPS = POSITIONS // P
-BLOCK = 2
-LOOKAHEAD = 8
+TILES = POSITIONS * BATCH // P
+ROUND = 4
+ROUNDS = TILES // ROUND
+BLOCK = 2 * ROUND
+LOOKAHEAD = 5
 
 FLOPS = 2 * POSITIONS * BATCH * WIDTH * FEATURES
 
@@ -63,11 +65,12 @@ def tile_selfattention_pa_t_kernel(
     tc, hidden_states, Wqkv, bqkv, rotary_pos_emb, out_0, out_1, out_2
 ):
     nc = tc.nc
-    x_dram = hidden_states.rearrange("(p s) b h -> p s b h", s=STEPS)
-    q_dram = out_0.rearrange("(p s) b n d -> p s (b n d)", s=STEPS)
-    k_dram = out_1.rearrange("(p s) b n d -> p s (b n d)", s=STEPS)
-    v_dram = out_2.rearrange("(p s) b n d -> p s (b n d)", s=STEPS)
-    rope_dram = rotary_pos_emb.rearrange("(p s) o j c -> p s (o j) c", s=STEPS)
+    per_partition = POSITIONS // P
+    x_dram = hidden_states.rearrange("(p s) b h -> p (s b) h", s=per_partition)
+    q_dram = out_0.rearrange("(p s) b n d -> p (s b) (n d)", s=per_partition)
+    k_dram = out_1.rearrange("(p s) b n d -> p (s b) (n d)", s=per_partition)
+    v_dram = out_2.rearrange("(p s) b n d -> p (s b) (n d)", s=per_partition)
+    rope_dram = rotary_pos_emb.rearrange("(p s) o j c -> p s (o j) c", s=per_partition)
 
     with ExitStack() as ctx:
         ctx.enter_context(tc.manual_schedule())
@@ -77,31 +80,38 @@ def tile_selfattention_pa_t_kernel(
         out_pool = ctx.enter_context(tc.tile_pool(name="out", bufs=3))
         scratch = ctx.enter_context(tc.tile_pool(name="scratch", bufs=2))
         turned_banks = ctx.enter_context(tc.psum_pool(name="turned", bufs=4))
-        acc_banks = ctx.enter_context(tc.psum_pool(name="acc", bufs=3))
-        spare_banks = ctx.enter_context(tc.psum_pool(name="spare", bufs=1))
+        acc_banks = ctx.enter_context(tc.psum_pool(name="acc", bufs=2))
 
         w_rows = const.tile([P, FEATURES // P, WIDTH], BF16)
         nc.sync.dma_start(out=w_rows[:], in_=Wqkv.rearrange("(i p) k -> p i k", p=P))
-        x_steps = {}
+        x_rounds = {}
 
-        def load_step(s):
-            x_rows = x_pool.tile([P, BATCH, WIDTH], BF16)
-            nc.sync.dma_start(out=x_rows[:], in_=x_dram[:, s])
-            x_steps[s] = x_rows
+        def load_round(r):
+            x_rows = x_pool.tile([P, ROUND, WIDTH], BF16)
+            nc.sync.dma_start(out=x_rows[:], in_=x_dram[:, r * ROUND : (r + 1) * ROUND, :])
+            x_rounds[r] = x_rows
 
-        for s in range(LOOKAHEAD):
-            load_step(s)
+        for r in range(LOOKAHEAD):
+            load_round(r)
 
-        rope_rows = const.tile([P, STEPS, PAIRS, 2], BF16)
+        rope_rows = const.tile([P, per_partition, PAIRS, 2], BF16)
         nc.scalar.dma_start(out=rope_rows[:], in_=rope_dram)
-        bias = const.tile([P, FEATURES], BF16)
-        nc.scalar.dma_start(out=bias[:], in_=bqkv.partition_broadcast(P))
+        bias_row = const.tile([P, FEATURES], BF16)
+        nc.vector.memset(bias_row[:], 0.0)
+        nc.scalar.dma_start(out=bias_row[0:1, :], in_=bqkv.rearrange("(o f) -> o f", o=1))
 
         identity = const.tile([P, P], F32)
         make_identity(nc, identity[:])
 
-        cos_sin = const.tile([P, STEPS, PAIRS, 2], F32)
-        minus_sin_cos = const.tile([P, STEPS, PAIRS, 2], F32)
+        ones = const.tile([P, P], BF16)
+        nc.vector.memset(ones[:], 1.0)
+        bias_bank = turned_banks.tile([P, FEATURES], F32, tag="turned")
+        nc.tensor.matmul(bias_bank[:], lhsT=ones[:], rhs=bias_row[:], start=True, stop=True)
+        bias = const.tile([P, FEATURES], F32)
+        nc.scalar.copy(out=bias[:], in_=bias_bank[:])
+
+        cos_sin = const.tile([P, per_partition, PAIRS, 2], F32)
+        minus_sin_cos = const.tile([P, per_partition, PAIRS, 2], F32)
         nc.vector.tensor_copy(out=cos_sin[:], in_=rope_rows[:])
         nc.vector.tensor_scalar_mul(
             out=minus_sin_cos[:, :, :, 0:1], in0=rope_rows[:, :, :, 1:2], scalar1=-1.0
@@ -125,101 +135,105 @@ def tile_selfattention_pa_t_kernel(
             in_=w_grouped[:].rearrange("p g n k -> p (g n k)"),
         )
 
-        grouped_steps, codes_steps, acc_steps, out_blocks = {}, {}, {}, {}
-        unread = spare_banks.tile([P, PASSES * FEATURES], F32)
+        grouped_rounds, codes_rounds, acc_rounds, out_blocks = {}, {}, {}, {}
 
-        def turn_step(s):
-            x_grouped = mx_pool.tile([P, BATCH, PASSES, P, PACK], BF16, align_bytes=64)
-            for b in range(BATCH):
+        def turn_round(r):
+            x_grouped = mx_pool.tile([P, ROUND, PASSES, P, PACK], BF16, align_bytes=64)
+            for t in range(ROUND):
                 k_onto_partitions(
                     nc,
                     turned_banks,
                     identity[:],
-                    x_steps[s][:, b, :].bitcast(F32),
-                    x_grouped[:, b].bitcast(F32),
+                    x_rounds[r][:, t, :].bitcast(F32),
+                    x_grouped[:, t].bitcast(F32),
                 )
-            grouped_steps[s] = x_grouped
+            grouped_rounds[r] = x_grouped
 
-        def quantise_step(s):
-            x_codes = mx_pool.tile([P, BATCH, PASSES, P], U32, align_bytes=64)
-            x_scales = mx_pool.tile([P, BATCH, PASSES, P], U8, align_bytes=64)
+        def quantise_round(r):
+            x_codes = mx_pool.tile([P, ROUND, PASSES, P], U32, align_bytes=64)
+            x_scales = mx_pool.tile([P, ROUND, PASSES, P], U8, align_bytes=64)
             nc.vector.quantize_mx(
-                out=x_codes[:].rearrange("p b g r -> p (b g r)").bitcast(FP8X4),
-                scales=x_scales[:].rearrange("p b g r -> p (b g r)"),
-                in_=grouped_steps[s][:].rearrange("p b g r k -> p (b g r k)"),
+                out=x_codes[:].rearrange("p t g r -> p (t g r)").bitcast(FP8X4),
+                scales=x_scales[:].rearrange("p t g r -> p (t g r)"),
+                in_=grouped_rounds[r][:].rearrange("p t g r k -> p (t g r k)"),
             )
-            codes_steps[s] = (x_codes, x_scales)
+            codes_rounds[r] = (x_codes, x_scales)
 
-        def multiply_step(s):
-            x_codes, x_scales = codes_steps[s]
-            acc = acc_banks.tile([P, BATCH, FEATURES], F32)
-            for b in range(BATCH):
-                for g in range(PASSES):
-                    nc.tensor.matmul_mx(
-                        out=acc[:, b, :],
-                        lhsT=x_codes[:, b, g, :].bitcast(FP8X4),
-                        lhsT_scale=x_scales[:, b, g, :],
-                        rhs=w_codes[:, g, :].bitcast(FP8X4),
-                        rhs_scale=w_scales[:, g, :],
-                        start=(g == 0),
-                        stop=(g == PASSES - 1),
-                    )
-            acc_steps[s] = acc
-            nc.tensor.matmul_mx(
-                out=unread[:],
-                lhsT=x_codes[:, 0, 0, :].bitcast(FP8X4),
-                lhsT_scale=x_scales[:, 0, 0, :],
-                rhs=w_codes[:].rearrange("p g n -> p (g n)").bitcast(FP8X4),
-                rhs_scale=w_scales[:].rearrange("p g n -> p (g n)"),
-                start=True,
-                stop=True,
+        def multiply_round(r):
+            x_codes, x_scales = codes_rounds[r]
+            acc_q = acc_banks.tile([P, ROUND, HALF], F32)
+            acc_kv = acc_banks.tile([P, ROUND, HALF], F32)
+            for t in range(ROUND):
+                for acc, first in ((acc_q, 0), (acc_kv, HALF)):
+                    for g in range(PASSES):
+                        nc.tensor.matmul_mx(
+                            out=acc[:, t, :],
+                            lhsT=x_codes[:, t, g, :].bitcast(FP8X4),
+                            lhsT_scale=x_scales[:, t, g, :],
+                            rhs=w_codes[:, g, first : first + HALF].bitcast(FP8X4),
+                            rhs_scale=w_scales[:, g, first : first + HALF],
+                            start=(g == 0),
+                            stop=(g == PASSES - 1),
+                        )
+            acc_rounds[r] = (acc_q, acc_kv)
+
+        def add_bias_round(r):
+            if r * ROUND % BLOCK == 0:
+                q_rows = out_pool.tile([P, BLOCK, HALF], F32)
+                kv_rows = out_pool.tile([P, 2, BLOCK, HEAD], F32)
+                out_blocks[r * ROUND // BLOCK] = (q_rows, kv_rows)
+            q_rows, kv_rows = out_blocks[r * ROUND // BLOCK]
+            acc_q, acc_kv = acc_rounds[r]
+            tiles = slice(r * ROUND % BLOCK, r * ROUND % BLOCK + ROUND)
+            nc.vector.tensor_tensor(
+                out=q_rows[:, tiles, :],
+                in0=acc_q[:],
+                in1=bias[:, 0:HALF].unsqueeze(1).to_broadcast([P, ROUND, HALF]),
+                op=ADD,
             )
-
-        def add_bias_step(s):
-            if s % BLOCK == 0:
-                q_rows = out_pool.tile([P, BLOCK, BATCH, Q_COLS], F32)
-                k_rows = out_pool.tile([P, BLOCK, BATCH, K_COLS], F32)
-                v_rows = out_pool.tile([P, BLOCK, BATCH, V_COLS], F32)
-                out_blocks[s // BLOCK] = (q_rows, k_rows, v_rows)
-            first = 0
-            for rows in out_blocks[s // BLOCK]:
-                cols = rows.shape[3]
-                nc.vector.tensor_tensor(
-                    out=rows[:, s % BLOCK],
-                    in0=acc_steps[s][:, :, first : first + cols],
-                    in1=bias[:, first : first + cols].unsqueeze(1).to_broadcast([P, BATCH, cols]),
-                    op=ADD,
-                )
-                first += cols
+            nc.vector.tensor_tensor(
+                out=kv_rows[:, :, tiles, :].rearrange("p r t d -> p t r d"),
+                in0=acc_kv[:].rearrange("p t (r d) -> p t r d", d=HEAD),
+                in1=bias[:, HALF:FEATURES]
+                .rearrange("p (r d) -> p r d", d=HEAD)
+                .unsqueeze(1)
+                .to_broadcast([P, ROUND, 2, HEAD]),
+                op=ADD,
+            )
 
         def rotate_and_store_block(c):
-            q_rows, k_rows, v_rows = out_blocks[c]
-            steps = slice(c * BLOCK, (c + 1) * BLOCK)
-            nc.sync.dma_start(out=v_dram[:, steps], in_=v_rows[:].rearrange("p i b c -> p i (b c)"))
+            q_rows, kv_rows = out_blocks[c]
+            tiles = slice(c * BLOCK, (c + 1) * BLOCK)
+            positions = slice(c * BLOCK // BATCH, (c + 1) * BLOCK // BATCH)
+            nc.sync.dma_start(out=v_dram[:, tiles, :], in_=kv_rows[:, 1])
             q_terms = rotation_terms(
                 nc,
                 scratch,
-                q_rows[:].rearrange("p i b (n d) -> p i (b n) d", d=HEAD),
-                cos_sin[:, steps],
-                minus_sin_cos[:, steps],
+                q_rows[:].rearrange("p (i b) (n d) -> p i (b n) d", b=BATCH, d=HEAD),
+                cos_sin[:, positions],
+                minus_sin_cos[:, positions],
             )
             k_terms = rotation_terms(
-                nc, scratch, k_rows[:], cos_sin[:, steps], minus_sin_cos[:, steps]
+                nc,
+                scratch,
+                kv_rows[:, 0].rearrange("p (i b) d -> p i b d", b=BATCH),
+                cos_sin[:, positions],
+                minus_sin_cos[:, positions],
             )
             for rotated, from_even, from_odd in (q_terms, k_terms):
                 nc.vector.tensor_tensor(out=rotated, in0=from_even[:], in1=from_odd[:], op=ADD)
-            nc.sync.dma_start(out=q_dram[:, steps], in_=q_rows[:].rearrange("p i b c -> p i (b c)"))
-            nc.sync.dma_start(out=k_dram[:, steps], in_=k_rows[:].rearrange("p i b c -> p i (b c)"))
+            nc.sync.dma_start(out=q_dram[:, tiles, :], in_=q_rows[:])
+            nc.sync.dma_start(out=k_dram[:, tiles, :], in_=kv_rows[:, 0])
 
-        for n in range(STEPS + 2):
-            if n + LOOKAHEAD < STEPS:
-                load_step(n + LOOKAHEAD)
-            if n < STEPS:
-                turn_step(n)
-            if 1 <= n <= STEPS:
-                quantise_step(n - 1)
-                multiply_step(n - 1)
+        for n in range(ROUNDS + 2):
+            if n + LOOKAHEAD < ROUNDS:
+                load_round(n + LOOKAHEAD)
+            if n < ROUNDS:
+                turn_round(n)
+            if 1 <= n <= ROUNDS:
+                quantise_round(n - 1)
+                multiply_round(n - 1)
             if n >= 2:
-                add_bias_step(n - 2)
-                if (n - 2) % BLOCK == BLOCK - 1:
-                    rotate_and_store_block((n - 2) // BLOCK)
+                add_bias_round(n - 2)
+                if (n - 2) * ROUND % BLOCK == BLOCK - ROUND:
+                    rotate_and_store_block((n - 2) * ROUND // BLOCK)

@@ -91,32 +91,34 @@ def tile_selfattention_pa_t_kernel(
             nc.sync.dma_start(out=x_rows[:], in_=x_dram[:, r * ROUND : (r + 1) * ROUND, :])
             x_rounds[r] = x_rows
 
-        for r in range(LOOKAHEAD):
-            load_round(r)
-
         rope_rows = const.tile([P, per_partition, PAIRS, 2], BF16)
-        nc.scalar.dma_start(out=rope_rows[:], in_=rope_dram)
         bias_row = const.tile([P, FEATURES], BF16)
         nc.vector.memset(bias_row[:], 0.0)
-        nc.scalar.dma_start(out=bias_row[0:1, :], in_=bqkv.rearrange("(o f) -> o f", o=1))
+        load_round(0)
+        nc.sync.dma_start(out=bias_row[0:1, :], in_=bqkv.rearrange("(o f) -> o f", o=1))
+        nc.sync.dma_start(out=rope_rows[:], in_=rope_dram)
+        for r in range(1, LOOKAHEAD):
+            load_round(r)
 
         identity = const.tile([P, P], F32)
         make_identity(nc, identity[:])
-
         ones = const.tile([P, P], BF16)
         nc.vector.memset(ones[:], 1.0)
-        bias_bank = turned_banks.tile([P, FEATURES], F32, tag="turned")
-        nc.tensor.matmul(bias_bank[:], lhsT=ones[:], rhs=bias_row[:], start=True, stop=True)
         bias = const.tile([P, FEATURES], F32)
-        nc.scalar.copy(out=bias[:], in_=bias_bank[:])
-
         cos_sin = const.tile([P, per_partition, PAIRS, 2], F32)
         minus_sin_cos = const.tile([P, per_partition, PAIRS, 2], F32)
-        nc.vector.tensor_copy(out=cos_sin[:], in_=rope_rows[:])
-        nc.vector.tensor_scalar_mul(
-            out=minus_sin_cos[:, :, :, 0:1], in0=rope_rows[:, :, :, 1:2], scalar1=-1.0
-        )
-        nc.vector.tensor_copy(out=minus_sin_cos[:, :, :, 1:2], in_=rope_rows[:, :, :, 0:1])
+
+        def spread_bias():
+            bias_bank = turned_banks.tile([P, FEATURES], F32, tag="turned")
+            nc.tensor.matmul(bias_bank[:], lhsT=ones[:], rhs=bias_row[:], start=True, stop=True)
+            nc.scalar.copy(out=bias[:], in_=bias_bank[:])
+
+        def make_angle_tables():
+            nc.vector.tensor_copy(out=cos_sin[:], in_=rope_rows[:])
+            nc.vector.tensor_scalar_mul(
+                out=minus_sin_cos[:, :, :, 0:1], in0=rope_rows[:, :, :, 1:2], scalar1=-1.0
+            )
+            nc.vector.tensor_copy(out=minus_sin_cos[:, :, :, 1:2], in_=rope_rows[:, :, :, 0:1])
 
         w_grouped = const.tile([P, PASSES, FEATURES, PACK], BF16, align_bytes=64)
         w_codes = const.tile([P, PASSES, FEATURES], U32, align_bytes=64)
@@ -230,9 +232,13 @@ def tile_selfattention_pa_t_kernel(
                 load_round(n + LOOKAHEAD)
             if n < ROUNDS:
                 turn_round(n)
+            if n == 0:
+                spread_bias()
             if 1 <= n <= ROUNDS:
                 quantise_round(n - 1)
                 multiply_round(n - 1)
+            if n == 1:
+                make_angle_tables()
             if n >= 2:
                 add_bias_round(n - 2)
                 if (n - 2) * ROUND % BLOCK == BLOCK - ROUND:

@@ -10,13 +10,16 @@ U8 = mybir.dt.uint8
 FP8X4 = mybir.dt.float8_e4m3fn_x4
 ADD = mybir.AluOpType.add
 MULT = mybir.AluOpType.mult
+IDENTITY = mybir.ActivationFunctionType.Identity
 
 P = 128
 POSITIONS, BATCH, WIDTH = 4096, 2, 1024
 HEAD = 64
+Q_HEADS = 2
 FEATURES = 4 * HEAD
-HALF = 2 * HEAD
+HALF = FEATURES // 2
 ROTATED = 32
+ROT_HEADS = Q_HEADS + 1
 PAIRS = ROTATED // 2
 
 PACK = 4
@@ -32,33 +35,13 @@ LOOKAHEAD = 5
 FLOPS = 2 * POSITIONS * BATCH * WIDTH * FEATURES
 
 
-def k_onto_partitions(nc, banks, identity, rows_words, grouped_words):
+def turn(nc, banks, identity, rows_words):
     bank = banks.tile([P, PASSES, HALVES, P], F32, tag="turned")
     for g in range(PASSES):
         for u in range(HALVES):
             first = (g * HALVES + u) * P
             nc.tensor.transpose(bank[:, g, u, :], rows_words[:, first : first + P], identity)
-    nc.scalar.copy(out=grouped_words, in_=bank[:].rearrange("p g u r -> p g r u"))
-
-
-def rotation_terms(nc, scratch, heads, cos_sin, minus_sin_cos):
-    shape = [P, heads.shape[1], heads.shape[2], PAIRS, 2]
-    rotated = heads[:, :, :, 0:ROTATED].rearrange("p i m (j e) -> p i m j e", e=2)
-    from_even = scratch.tile(shape, F32, tag="from_even%d" % shape[2])
-    from_odd = scratch.tile(shape, F32, tag="from_odd%d" % shape[2])
-    nc.vector.tensor_tensor(
-        out=from_even[:],
-        in0=rotated[:, :, :, :, 0:1].to_broadcast(shape),
-        in1=cos_sin.unsqueeze(2).to_broadcast(shape),
-        op=MULT,
-    )
-    nc.vector.tensor_tensor(
-        out=from_odd[:],
-        in0=rotated[:, :, :, :, 1:2].to_broadcast(shape),
-        in1=minus_sin_cos.unsqueeze(2).to_broadcast(shape),
-        op=MULT,
-    )
-    return rotated, from_even, from_odd
+    return bank
 
 
 def tile_selfattention_pa_t_kernel(
@@ -80,7 +63,9 @@ def tile_selfattention_pa_t_kernel(
         out_pool = ctx.enter_context(tc.tile_pool(name="out", bufs=3))
         scratch = ctx.enter_context(tc.tile_pool(name="scratch", bufs=2))
         turned_banks = ctx.enter_context(tc.psum_pool(name="turned", bufs=4))
-        acc_banks = ctx.enter_context(tc.psum_pool(name="acc", bufs=2))
+        fm_banks = ctx.enter_context(tc.psum_pool(name="by_feature", bufs=1))
+        back_banks = ctx.enter_context(tc.psum_pool(name="back", bufs=1))
+        tm_banks = ctx.enter_context(tc.psum_pool(name="by_token", bufs=2))
 
         w_rows = const.tile([P, FEATURES // P, WIDTH], BF16)
         nc.sync.dma_start(out=w_rows[:], in_=Wqkv.rearrange("(i p) k -> p i k", p=P))
@@ -92,10 +77,9 @@ def tile_selfattention_pa_t_kernel(
             x_rounds[r] = x_rows
 
         rope_rows = const.tile([P, per_partition, PAIRS, 2], BF16)
-        bias_row = const.tile([P, FEATURES], BF16)
-        nc.vector.memset(bias_row[:], 0.0)
+        bias_in = const.tile([P, FEATURES], BF16)
         load_round(0)
-        nc.sync.dma_start(out=bias_row[0:1, :], in_=bqkv.rearrange("(o f) -> o f", o=1))
+        nc.sync.dma_start(out=bias_in[0:1, :], in_=bqkv.rearrange("(o f) -> o f", o=1))
         nc.sync.dma_start(out=rope_rows[:], in_=rope_dram)
         for r in range(1, LOOKAHEAD):
             load_round(r)
@@ -104,142 +88,236 @@ def tile_selfattention_pa_t_kernel(
         make_identity(nc, identity[:])
         ones = const.tile([P, P], BF16)
         nc.vector.memset(ones[:], 1.0)
-        bias = const.tile([P, FEATURES], F32)
-        cos_sin = const.tile([P, per_partition, PAIRS, 2], F32)
-        minus_sin_cos = const.tile([P, per_partition, PAIRS, 2], F32)
+
+        def in_order(columns):
+            parts = columns.rearrange("p (s c) w -> p s c w", s=2)
+            q = parts[:, :, 0 : Q_HEADS * ROTATED].rearrange("p s (n r) w -> p n s r w", r=ROTATED)
+            return q, parts[:, :, Q_HEADS * ROTATED : HALF]
+
+        bias_row = const.tile([P, FEATURES, 1], BF16)
+        nc.vector.memset(bias_row[:], 0.0)
+        bias_tm = const.tile([P, HALF], F32)
+        bias_fm = const.tile([P, 1], F32)
 
         def spread_bias():
-            bias_bank = turned_banks.tile([P, FEATURES], F32, tag="turned")
-            nc.tensor.matmul(bias_bank[:], lhsT=ones[:], rhs=bias_row[:], start=True, stop=True)
-            nc.scalar.copy(out=bias[:], in_=bias_bank[:])
+            q, kv = in_order(bias_row[0:1])
+            nc.vector.tensor_copy(
+                out=q, in_=bias_in[0:1, 0:HALF].rearrange("p (n s r w) -> p n s r w", n=Q_HEADS, s=2, w=1)
+            )
+            nc.vector.tensor_copy(
+                out=kv, in_=bias_in[0:1, HALF:FEATURES].rearrange("p (s c w) -> p s c w", s=2, w=1)
+            )
+            row = bias_row[:].rearrange("p f w -> p (f w)")
+            bank = turned_banks.tile([P, HALF + 1], F32, tag="turned")
+            nc.tensor.matmul(bank[:, 0:HALF], lhsT=ones[:], rhs=row[:, HALF:FEATURES], start=True, stop=True)
+            nc.tensor.matmul(bank[:, HALF : HALF + 1], lhsT=row[:, 0:HALF], rhs=ones[:, 0:1], start=True, stop=True)
+            nc.scalar.copy(out=bias_tm[:], in_=bank[:, 0:HALF])
+            nc.scalar.copy(out=bias_fm[:], in_=bank[:, HALF : HALF + 1])
+
+        cos_sin = const.tile([P, TILES, PAIRS, 2], BF16)
+        minus_sin_cos = const.tile([P, TILES, PAIRS, 2], BF16)
 
         def make_angle_tables():
-            nc.vector.tensor_copy(out=cos_sin[:], in_=rope_rows[:])
-            nc.vector.tensor_scalar_mul(
-                out=minus_sin_cos[:, :, :, 0:1], in0=rope_rows[:, :, :, 1:2], scalar1=-1.0
+            def by_position(table):
+                return table.rearrange("p (i b) j e -> p i b j e", b=BATCH)
+
+            shape = [P, per_partition, BATCH, PAIRS]
+            sin = rope_rows[:, :, :, 1].unsqueeze(2).to_broadcast(shape)
+            cos = rope_rows[:, :, :, 0].unsqueeze(2).to_broadcast(shape)
+            nc.vector.tensor_copy(
+                out=cos_sin[:].rearrange("p (i b) j e -> p i b (j e)", b=BATCH),
+                in_=rope_rows[:]
+                .rearrange("p i j e -> p i (j e)")
+                .unsqueeze(2)
+                .to_broadcast([P, per_partition, BATCH, 2 * PAIRS]),
             )
-            nc.vector.tensor_copy(out=minus_sin_cos[:, :, :, 1:2], in_=rope_rows[:, :, :, 0:1])
+            nc.vector.tensor_scalar_mul(
+                out=by_position(minus_sin_cos[:])[:, :, :, :, 0], in0=sin, scalar1=-1.0
+            )
+            nc.vector.tensor_copy(out=by_position(minus_sin_cos[:])[:, :, :, :, 1], in_=cos)
 
         w_grouped = const.tile([P, PASSES, FEATURES, PACK], BF16, align_bytes=64)
         w_codes = const.tile([P, PASSES, FEATURES], U32, align_bytes=64)
         w_scales = const.tile([P, PASSES, FEATURES], U8, align_bytes=64)
         for i in range(FEATURES // P):
-            k_onto_partitions(
-                nc,
-                turned_banks,
-                identity[:],
-                w_rows[:, i, :].bitcast(F32),
-                w_grouped[:].bitcast(F32)[:, :, i * P : (i + 1) * P, :],
-            )
+            bank = turn(nc, turned_banks, identity[:], w_rows[:, i, :].bitcast(F32))
+            for g in range(PASSES):
+                words = bank[:, g].rearrange("p u f -> p f u")
+                q, kv = in_order(w_grouped[:].bitcast(F32)[:, g])
+                if i == 0:
+                    nc.scalar.copy(out=q, in_=words.rearrange("p (n s r) u -> p n s r u", n=Q_HEADS, s=2))
+                else:
+                    nc.scalar.copy(out=kv, in_=words.rearrange("p (s c) u -> p s c u", s=2))
         nc.vector.quantize_mx(
             out=w_codes[:].rearrange("p g n -> p (g n)").bitcast(FP8X4),
             scales=w_scales[:].rearrange("p g n -> p (g n)"),
             in_=w_grouped[:].rearrange("p g n k -> p (g n k)"),
         )
 
-        grouped_rounds, codes_rounds, acc_rounds, out_blocks = {}, {}, {}, {}
+        grouped_rounds, codes_rounds, fm_rounds, tm_rounds = {}, {}, {}, {}
+        back_rounds, term_rounds, out_blocks = {}, {}, {}
 
-        def turn_round(r):
-            x_grouped = mx_pool.tile([P, ROUND, PASSES, P, PACK], BF16, align_bytes=64)
-            for t in range(ROUND):
-                k_onto_partitions(
-                    nc,
-                    turned_banks,
-                    identity[:],
-                    x_rounds[r][:, t, :].bitcast(F32),
-                    x_grouped[:, t].bitcast(F32),
+        def turn_tiles(r, tiles):
+            if r not in grouped_rounds:
+                x_grouped = mx_pool.tile([P, PASSES, ROUND, P, PACK], BF16, align_bytes=64)
+                grouped_rounds[r] = x_grouped
+            for t in tiles:
+                bank = turn(nc, turned_banks, identity[:], x_rounds[r][:, t, :].bitcast(F32))
+                nc.scalar.copy(
+                    out=grouped_rounds[r][:].bitcast(F32)[:, :, t],
+                    in_=bank[:].rearrange("p g u r -> p g r u"),
                 )
-            grouped_rounds[r] = x_grouped
 
-        def quantise_round(r):
-            x_codes = mx_pool.tile([P, ROUND, PASSES, P], U32, align_bytes=64)
-            x_scales = mx_pool.tile([P, ROUND, PASSES, P], U8, align_bytes=64)
+        def quantise(r):
+            x_codes = mx_pool.tile([P, PASSES, ROUND * P], U32, align_bytes=64)
+            x_scales = mx_pool.tile([P, PASSES, ROUND * P], U8, align_bytes=64)
             nc.vector.quantize_mx(
-                out=x_codes[:].rearrange("p t g r -> p (t g r)").bitcast(FP8X4),
-                scales=x_scales[:].rearrange("p t g r -> p (t g r)"),
-                in_=grouped_rounds[r][:].rearrange("p t g r k -> p (t g r k)"),
+                out=x_codes[:].rearrange("p g n -> p (g n)").bitcast(FP8X4),
+                scales=x_scales[:].rearrange("p g n -> p (g n)"),
+                in_=grouped_rounds[r][:].rearrange("p g t n k -> p (g t n k)"),
             )
             codes_rounds[r] = (x_codes, x_scales)
 
-        def multiply_round(r):
+        def multiply_by_feature(r):
             x_codes, x_scales = codes_rounds[r]
-            acc_q = acc_banks.tile([P, ROUND, HALF], F32)
-            acc_kv = acc_banks.tile([P, ROUND, HALF], F32)
+            bank = fm_banks.tile([P, ROUND * P], F32)
+            for g in range(PASSES):
+                nc.tensor.matmul_mx(
+                    out=bank[:],
+                    lhsT=w_codes[:, g, 0:HALF].bitcast(FP8X4),
+                    lhsT_scale=w_scales[:, g, 0:HALF],
+                    rhs=x_codes[:, g, :].bitcast(FP8X4),
+                    rhs_scale=x_scales[:, g, :],
+                    start=(g == 0),
+                    stop=(g == PASSES - 1),
+                )
+            fm_rows = scratch.tile([P, ROUND * P], F32)
+            nc.scalar.activation(out=fm_rows[:], in_=bank[:], func=IDENTITY, bias=bias_fm[:, 0:1])
+            fm_rounds[r] = fm_rows
+
+        def multiply_by_token(r):
+            x_codes, x_scales = codes_rounds[r]
+            bank = tm_banks.tile([P, ROUND, HALF], F32)
             for t in range(ROUND):
-                for acc, first in ((acc_q, 0), (acc_kv, HALF)):
-                    for g in range(PASSES):
-                        nc.tensor.matmul_mx(
-                            out=acc[:, t, :],
-                            lhsT=x_codes[:, t, g, :].bitcast(FP8X4),
-                            lhsT_scale=x_scales[:, t, g, :],
-                            rhs=w_codes[:, g, first : first + HALF].bitcast(FP8X4),
-                            rhs_scale=w_scales[:, g, first : first + HALF],
-                            start=(g == 0),
-                            stop=(g == PASSES - 1),
-                        )
-            acc_rounds[r] = (acc_q, acc_kv)
+                for g in range(PASSES):
+                    nc.tensor.matmul_mx(
+                        out=bank[:, t, :],
+                        lhsT=x_codes[:, g, t * P : (t + 1) * P].bitcast(FP8X4),
+                        lhsT_scale=x_scales[:, g, t * P : (t + 1) * P],
+                        rhs=w_codes[:, g, HALF:FEATURES].bitcast(FP8X4),
+                        rhs_scale=w_scales[:, g, HALF:FEATURES],
+                        start=(g == 0),
+                        stop=(g == PASSES - 1),
+                    )
+            tm_rounds[r] = bank
 
-        def add_bias_round(r):
-            if r * ROUND % BLOCK == 0:
-                q_rows = out_pool.tile([P, BLOCK, HALF], F32)
-                kv_rows = out_pool.tile([P, 2, BLOCK, HEAD], F32)
-                out_blocks[r * ROUND // BLOCK] = (q_rows, kv_rows)
-            q_rows, kv_rows = out_blocks[r * ROUND // BLOCK]
-            acc_q, acc_kv = acc_rounds[r]
-            tiles = slice(r * ROUND % BLOCK, r * ROUND % BLOCK + ROUND)
+        def turn_back(r):
+            bank = back_banks.tile([P, ROUND, HALF], F32)
+            for t in range(ROUND):
+                nc.tensor.transpose(bank[:, t, :], fm_rounds[r][:, t * P : (t + 1) * P], identity[:])
+            back_rounds[r] = bank
+
+        def rows_of(r):
+            block, first = divmod(r * ROUND, BLOCK)
+            if block not in out_blocks:
+                q_rows = out_pool.tile([P, BLOCK, Q_HEADS, HEAD], F32)
+                k_rows = out_pool.tile([P, BLOCK, HEAD], F32)
+                v_rows = out_pool.tile([P, BLOCK, HEAD], F32)
+                out_blocks[block] = (q_rows, k_rows, v_rows)
+            q_rows, k_rows, v_rows = out_blocks[block]
+            tiles = slice(first, first + ROUND)
+            return q_rows[:, tiles], k_rows[:, tiles], v_rows[:, tiles]
+
+        def rest_of_q(r):
+            shape = [P, ROUND, Q_HEADS, HEAD - ROTATED]
+            first_v = Q_HEADS * (HEAD - ROTATED)
             nc.vector.tensor_tensor(
-                out=q_rows[:, tiles, :],
-                in0=acc_q[:],
-                in1=bias[:, 0:HALF].unsqueeze(1).to_broadcast([P, ROUND, HALF]),
-                op=ADD,
-            )
-            nc.vector.tensor_tensor(
-                out=kv_rows[:, :, tiles, :].rearrange("p r t d -> p t r d"),
-                in0=acc_kv[:].rearrange("p t (r d) -> p t r d", d=HEAD),
-                in1=bias[:, HALF:FEATURES]
-                .rearrange("p (r d) -> p r d", d=HEAD)
+                out=rows_of(r)[0][:, :, :, ROTATED:HEAD],
+                in0=tm_rounds[r][:, :, 0:first_v].rearrange("p t (n d) -> p t n d", n=Q_HEADS),
+                in1=bias_tm[:, 0:first_v]
+                .rearrange("p (n d) -> p n d", n=Q_HEADS)
                 .unsqueeze(1)
-                .to_broadcast([P, ROUND, 2, HEAD]),
+                .to_broadcast(shape),
                 op=ADD,
             )
 
-        def rotate_and_store_block(c):
-            q_rows, kv_rows = out_blocks[c]
+        def values(r):
+            nc.vector.tensor_tensor(
+                out=rows_of(r)[2],
+                in0=tm_rounds[r][:, :, HALF - HEAD : HALF],
+                in1=bias_tm[:, HALF - HEAD : HALF].unsqueeze(1).to_broadcast([P, ROUND, HEAD]),
+                op=ADD,
+            )
+
+        def rest_of_k(r):
+            nc.scalar.copy(
+                out=rows_of(r)[1][:, :, ROTATED:HEAD],
+                in_=back_rounds[r][:, :, ROT_HEADS * ROTATED : HALF],
+            )
+
+        def rotation_terms(r):
+            shape = [P, ROUND, ROT_HEADS, PAIRS, 2]
+            tiles = slice(r * ROUND, (r + 1) * ROUND)
+            pairs = back_rounds[r][:, :, 0 : ROT_HEADS * ROTATED].rearrange(
+                "p t (h j e) -> p t h j e", h=ROT_HEADS, e=2
+            )
+            from_even = scratch.tile(shape, F32)
+            from_odd = scratch.tile(shape, F32)
+            for term, e, table in ((from_even, 0, cos_sin), (from_odd, 1, minus_sin_cos)):
+                nc.vector.tensor_tensor(
+                    out=term[:],
+                    in0=pairs[:, :, :, :, e : e + 1].to_broadcast(shape),
+                    in1=table[:, tiles].unsqueeze(2).to_broadcast(shape),
+                    op=MULT,
+                )
+            term_rounds[r] = (from_even, from_odd)
+
+        def rotate(r):
+            q_rows, k_rows, v_rows = rows_of(r)
+            even, odd = [t[:].rearrange("p t h j e -> p t h (j e)") for t in term_rounds[r]]
+            nc.vector.tensor_tensor(
+                out=q_rows[:, :, :, 0:ROTATED],
+                in0=even[:, :, 0:Q_HEADS],
+                in1=odd[:, :, 0:Q_HEADS],
+                op=ADD,
+            )
+            nc.vector.tensor_tensor(
+                out=k_rows[:, :, 0:ROTATED], in0=even[:, :, Q_HEADS], in1=odd[:, :, Q_HEADS], op=ADD
+            )
+
+        def store_block(c):
+            q_rows, k_rows, v_rows = out_blocks[c]
             tiles = slice(c * BLOCK, (c + 1) * BLOCK)
-            positions = slice(c * BLOCK // BATCH, (c + 1) * BLOCK // BATCH)
-            nc.sync.dma_start(out=v_dram[:, tiles, :], in_=kv_rows[:, 1])
-            q_terms = rotation_terms(
-                nc,
-                scratch,
-                q_rows[:].rearrange("p (i b) (n d) -> p i (b n) d", b=BATCH, d=HEAD),
-                cos_sin[:, positions],
-                minus_sin_cos[:, positions],
+            nc.sync.dma_start(out=v_dram[:, tiles, :], in_=v_rows[:])
+            nc.sync.dma_start(
+                out=q_dram[:, tiles, :], in_=q_rows[:].rearrange("p t n d -> p t (n d)")
             )
-            k_terms = rotation_terms(
-                nc,
-                scratch,
-                kv_rows[:, 0].rearrange("p (i b) d -> p i b d", b=BATCH),
-                cos_sin[:, positions],
-                minus_sin_cos[:, positions],
-            )
-            for rotated, from_even, from_odd in (q_terms, k_terms):
-                nc.vector.tensor_tensor(out=rotated, in0=from_even[:], in1=from_odd[:], op=ADD)
-            nc.sync.dma_start(out=q_dram[:, tiles, :], in_=q_rows[:])
-            nc.sync.dma_start(out=k_dram[:, tiles, :], in_=kv_rows[:, 0])
+            nc.sync.dma_start(out=k_dram[:, tiles, :], in_=k_rows[:])
 
         for n in range(ROUNDS + 2):
             if n + LOOKAHEAD < ROUNDS:
                 load_round(n + LOOKAHEAD)
+            if n >= 2:
+                turn_back(n - 2)
+                rest_of_q(n - 2)
+            if 1 <= n <= ROUNDS:
+                quantise(n - 1)
             if n < ROUNDS:
-                turn_round(n)
+                turn_tiles(n, (0, 1))
             if n == 0:
                 spread_bias()
             if 1 <= n <= ROUNDS:
-                quantise_round(n - 1)
-                multiply_round(n - 1)
+                multiply_by_feature(n - 1)
+            if n < ROUNDS:
+                turn_tiles(n, (2, 3))
             if n == 1:
                 make_angle_tables()
             if n >= 2:
-                add_bias_round(n - 2)
-                if (n - 2) * ROUND % BLOCK == BLOCK - ROUND:
-                    rotate_and_store_block((n - 2) * ROUND // BLOCK)
+                rotation_terms(n - 2)
+                values(n - 2)
+                rotate(n - 2)
+                rest_of_k(n - 2)
+                if (n - 1) * ROUND % BLOCK == 0:
+                    store_block((n - 2) * ROUND // BLOCK)
+            if 1 <= n <= ROUNDS:
+                multiply_by_token(n - 1)

@@ -62,9 +62,9 @@ def tile_selfattention_pa_t_kernel(
         mx_pool = ctx.enter_context(tc.tile_pool(name="mx", bufs=3))
         out_pool = ctx.enter_context(tc.tile_pool(name="out", bufs=3))
         scratch = ctx.enter_context(tc.tile_pool(name="scratch", bufs=2))
-        turned_banks = ctx.enter_context(tc.psum_pool(name="turned", bufs=4))
+        turned_banks = ctx.enter_context(tc.psum_pool(name="turned", bufs=3))
         fm_banks = ctx.enter_context(tc.psum_pool(name="by_feature", bufs=1))
-        back_banks = ctx.enter_context(tc.psum_pool(name="back", bufs=1))
+        back_banks = ctx.enter_context(tc.psum_pool(name="back", bufs=2))
         tm_banks = ctx.enter_context(tc.psum_pool(name="by_token", bufs=2))
 
         w_rows = const.tile([P, FEATURES // P, WIDTH], BF16)
@@ -294,30 +294,30 @@ def tile_selfattention_pa_t_kernel(
             )
             nc.sync.dma_start(out=k_dram[:, tiles, :], in_=k_rows[:])
 
-        for n in range(ROUNDS + 2):
+        for n in range(ROUNDS + 3):
             if n + LOOKAHEAD < ROUNDS:
                 load_round(n + LOOKAHEAD)
-            if n >= 2:
-                turn_back(n - 2)
-                rest_of_q(n - 2)
-            if 1 <= n <= ROUNDS:
-                quantise(n - 1)
+            if n >= 3:
+                turn_back(n - 3)
+                rest_of_q(n - 3)
+                rotation_terms(n - 3)
+                values(n - 3)
             if n < ROUNDS:
                 turn_tiles(n, (0, 1))
+            if 1 <= n <= ROUNDS:
+                quantise(n - 1)
             if n == 0:
                 spread_bias()
-            if 1 <= n <= ROUNDS:
-                multiply_by_feature(n - 1)
+            if 2 <= n <= ROUNDS + 1:
+                multiply_by_feature(n - 2)
             if n < ROUNDS:
                 turn_tiles(n, (2, 3))
             if n == 1:
                 make_angle_tables()
-            if n >= 2:
-                rotation_terms(n - 2)
-                values(n - 2)
-                rotate(n - 2)
-                rest_of_k(n - 2)
-                if (n - 1) * ROUND % BLOCK == 0:
-                    store_block((n - 2) * ROUND // BLOCK)
-            if 1 <= n <= ROUNDS:
-                multiply_by_token(n - 1)
+            if n >= 3:
+                rotate(n - 3)
+                rest_of_k(n - 3)
+                if (n - 2) * ROUND % BLOCK == 0:
+                    store_block((n - 3) * ROUND // BLOCK)
+            if 2 <= n <= ROUNDS + 1:
+                multiply_by_token(n - 2)

@@ -28,15 +28,18 @@ HALVES = 2
 
 TILES = POSITIONS * BATCH // P
 ROUND = 4
-ROUNDS = TILES // ROUND
 BLOCK = 2 * ROUND
-LOOKAHEAD = 5
+ENDS = [ROUND // 2, ROUND // 2]
+ROUND_TILES = ENDS + [ROUND] * (TILES // ROUND - 2) + ENDS
+ROUNDS = len(ROUND_TILES)
+FIRST_TILES = [sum(ROUND_TILES[:r]) for r in range(ROUNDS)]
+LOOKAHEAD = 6
 
 FLOPS = 2 * POSITIONS * BATCH * WIDTH * FEATURES
 
 
-def turn(nc, banks, identity, rows_words):
-    bank = banks.tile([P, PASSES, HALVES, P], F32, tag="turned")
+def turn(nc, banks, tag, identity, rows_words):
+    bank = banks.tile([P, PASSES, HALVES, P], F32, tag=tag)
     for g in range(PASSES):
         for u in range(HALVES):
             first = (g * HALVES + u) * P
@@ -67,21 +70,27 @@ def tile_selfattention_pa_t_kernel(
         back_banks = ctx.enter_context(tc.psum_pool(name="back", bufs=2))
         tm_banks = ctx.enter_context(tc.psum_pool(name="by_token", bufs=2))
 
-        w_rows = const.tile([P, FEATURES // P, WIDTH], BF16)
-        nc.sync.dma_start(out=w_rows[:], in_=Wqkv.rearrange("(i p) k -> p i k", p=P))
         x_rounds = {}
 
         def load_round(r):
-            x_rows = x_pool.tile([P, ROUND, WIDTH], BF16)
-            nc.sync.dma_start(out=x_rows[:], in_=x_dram[:, r * ROUND : (r + 1) * ROUND, :])
+            count, first = ROUND_TILES[r], FIRST_TILES[r]
+            x_rows = x_pool.tile([P, count, WIDTH], BF16)
+            piece = 1 if r == 0 else 2 if r <= 3 else count
+            for t in range(0, count, piece):
+                nc.sync.dma_start(
+                    out=x_rows[:, t : t + piece], in_=x_dram[:, first + t : first + t + piece, :]
+                )
             x_rounds[r] = x_rows
 
         rope_rows = const.tile([P, per_partition, PAIRS, 2], BF16)
         bias_in = const.tile([P, FEATURES], BF16)
-        load_round(0)
+        w_rows = const.tile([P, FEATURES // P, WIDTH], BF16)
         nc.sync.dma_start(out=bias_in[0:1, :], in_=bqkv.rearrange("(o f) -> o f", o=1))
+        load_round(0)
+        nc.sync.dma_start(out=w_rows[:], in_=Wqkv.rearrange("(i p) k -> p i k", p=P))
+        load_round(1)
         nc.sync.dma_start(out=rope_rows[:], in_=rope_dram)
-        for r in range(1, LOOKAHEAD):
+        for r in range(2, LOOKAHEAD):
             load_round(r)
 
         identity = const.tile([P, P], F32)
@@ -108,7 +117,7 @@ def tile_selfattention_pa_t_kernel(
                 out=kv, in_=bias_in[0:1, HALF:FEATURES].rearrange("p (s c w) -> p s c w", s=2, w=1)
             )
             row = bias_row[:].rearrange("p f w -> p (f w)")
-            bank = turned_banks.tile([P, HALF + 1], F32, tag="turned")
+            bank = back_banks.tile([P, HALF + 1], F32, tag="back")
             nc.tensor.matmul(bank[:, 0:HALF], lhsT=ones[:], rhs=row[:, HALF:FEATURES], start=True, stop=True)
             nc.tensor.matmul(bank[:, HALF : HALF + 1], lhsT=row[:, 0:HALF], rhs=ones[:, 0:1], start=True, stop=True)
             nc.scalar.copy(out=bias_tm[:], in_=bank[:, 0:HALF])
@@ -139,38 +148,46 @@ def tile_selfattention_pa_t_kernel(
         w_grouped = const.tile([P, PASSES, FEATURES, PACK], BF16, align_bytes=64)
         w_codes = const.tile([P, PASSES, FEATURES], U32, align_bytes=64)
         w_scales = const.tile([P, PASSES, FEATURES], U8, align_bytes=64)
-        for i in range(FEATURES // P):
-            bank = turn(nc, turned_banks, identity[:], w_rows[:, i, :].bitcast(F32))
-            for g in range(PASSES):
-                words = bank[:, g].rearrange("p u f -> p f u")
-                q, kv = in_order(w_grouped[:].bitcast(F32)[:, g])
-                if i == 0:
-                    nc.scalar.copy(out=q, in_=words.rearrange("p (n s r) u -> p n s r u", n=Q_HEADS, s=2))
-                else:
-                    nc.scalar.copy(out=kv, in_=words.rearrange("p (s c) u -> p s c u", s=2))
-        nc.vector.quantize_mx(
-            out=w_codes[:].rearrange("p g n -> p (g n)").bitcast(FP8X4),
-            scales=w_scales[:].rearrange("p g n -> p (g n)"),
-            in_=w_grouped[:].rearrange("p g n k -> p (g n k)"),
-        )
+
+        def turn_weights():
+            for i in range(FEATURES // P):
+                bank = turn(nc, tm_banks, "by_token", identity[:], w_rows[:, i, :].bitcast(F32))
+                for g in range(PASSES):
+                    words = bank[:, g].rearrange("p u f -> p f u")
+                    q, kv = in_order(w_grouped[:].bitcast(F32)[:, g])
+                    if i == 0:
+                        nc.vector.tensor_copy(
+                            out=q, in_=words.rearrange("p (n s r) u -> p n s r u", n=Q_HEADS, s=2)
+                        )
+                    else:
+                        nc.vector.tensor_copy(
+                            out=kv, in_=words.rearrange("p (s c) u -> p s c u", s=2)
+                        )
+
+        def quantise_weights():
+            nc.vector.quantize_mx(
+                out=w_codes[:].rearrange("p g n -> p (g n)").bitcast(FP8X4),
+                scales=w_scales[:].rearrange("p g n -> p (g n)"),
+                in_=w_grouped[:].rearrange("p g n k -> p (g n k)"),
+            )
 
         grouped_rounds, codes_rounds, fm_rounds, tm_rounds = {}, {}, {}, {}
         back_rounds, term_rounds, out_blocks = {}, {}, {}
 
         def turn_tiles(r, tiles):
             if r not in grouped_rounds:
-                x_grouped = mx_pool.tile([P, PASSES, ROUND, P, PACK], BF16, align_bytes=64)
+                x_grouped = mx_pool.tile([P, PASSES, ROUND_TILES[r], P, PACK], BF16, align_bytes=64)
                 grouped_rounds[r] = x_grouped
             for t in tiles:
-                bank = turn(nc, turned_banks, identity[:], x_rounds[r][:, t, :].bitcast(F32))
+                bank = turn(nc, turned_banks, "turned", identity[:], x_rounds[r][:, t, :].bitcast(F32))
                 nc.scalar.copy(
                     out=grouped_rounds[r][:].bitcast(F32)[:, :, t],
                     in_=bank[:].rearrange("p g u r -> p g r u"),
                 )
 
         def quantise(r):
-            x_codes = mx_pool.tile([P, PASSES, ROUND * P], U32, align_bytes=64)
-            x_scales = mx_pool.tile([P, PASSES, ROUND * P], U8, align_bytes=64)
+            x_codes = mx_pool.tile([P, PASSES, ROUND_TILES[r] * P], U32, align_bytes=64)
+            x_scales = mx_pool.tile([P, PASSES, ROUND_TILES[r] * P], U8, align_bytes=64)
             nc.vector.quantize_mx(
                 out=x_codes[:].rearrange("p g n -> p (g n)").bitcast(FP8X4),
                 scales=x_scales[:].rearrange("p g n -> p (g n)"),
@@ -180,7 +197,7 @@ def tile_selfattention_pa_t_kernel(
 
         def multiply_by_feature(r):
             x_codes, x_scales = codes_rounds[r]
-            bank = fm_banks.tile([P, ROUND * P], F32)
+            bank = fm_banks.tile([P, ROUND_TILES[r] * P], F32)
             for g in range(PASSES):
                 nc.tensor.matmul_mx(
                     out=bank[:],
@@ -191,14 +208,14 @@ def tile_selfattention_pa_t_kernel(
                     start=(g == 0),
                     stop=(g == PASSES - 1),
                 )
-            fm_rows = scratch.tile([P, ROUND * P], F32)
+            fm_rows = scratch.tile([P, ROUND_TILES[r] * P], F32)
             nc.scalar.activation(out=fm_rows[:], in_=bank[:], func=IDENTITY, bias=bias_fm[:, 0:1])
             fm_rounds[r] = fm_rows
 
         def multiply_by_token(r):
             x_codes, x_scales = codes_rounds[r]
-            bank = tm_banks.tile([P, ROUND, HALF], F32)
-            for t in range(ROUND):
+            bank = tm_banks.tile([P, ROUND_TILES[r], HALF], F32, tag="by_token")
+            for t in range(ROUND_TILES[r]):
                 for g in range(PASSES):
                     nc.tensor.matmul_mx(
                         out=bank[:, t, :],
@@ -212,24 +229,24 @@ def tile_selfattention_pa_t_kernel(
             tm_rounds[r] = bank
 
         def turn_back(r):
-            bank = back_banks.tile([P, ROUND, HALF], F32)
-            for t in range(ROUND):
+            bank = back_banks.tile([P, ROUND_TILES[r], HALF], F32, tag="back")
+            for t in range(ROUND_TILES[r]):
                 nc.tensor.transpose(bank[:, t, :], fm_rounds[r][:, t * P : (t + 1) * P], identity[:])
             back_rounds[r] = bank
 
         def rows_of(r):
-            block, first = divmod(r * ROUND, BLOCK)
+            block, first = divmod(FIRST_TILES[r], BLOCK)
             if block not in out_blocks:
                 q_rows = out_pool.tile([P, BLOCK, Q_HEADS, HEAD], F32)
                 k_rows = out_pool.tile([P, BLOCK, HEAD], F32)
                 v_rows = out_pool.tile([P, BLOCK, HEAD], F32)
                 out_blocks[block] = (q_rows, k_rows, v_rows)
             q_rows, k_rows, v_rows = out_blocks[block]
-            tiles = slice(first, first + ROUND)
+            tiles = slice(first, first + ROUND_TILES[r])
             return q_rows[:, tiles], k_rows[:, tiles], v_rows[:, tiles]
 
         def rest_of_q(r):
-            shape = [P, ROUND, Q_HEADS, HEAD - ROTATED]
+            shape = [P, ROUND_TILES[r], Q_HEADS, HEAD - ROTATED]
             first_v = Q_HEADS * (HEAD - ROTATED)
             nc.vector.tensor_tensor(
                 out=rows_of(r)[0][:, :, :, ROTATED:HEAD],
@@ -245,7 +262,7 @@ def tile_selfattention_pa_t_kernel(
             nc.vector.tensor_tensor(
                 out=rows_of(r)[2],
                 in0=tm_rounds[r][:, :, HALF - HEAD : HALF],
-                in1=bias_tm[:, HALF - HEAD : HALF].unsqueeze(1).to_broadcast([P, ROUND, HEAD]),
+                in1=bias_tm[:, HALF - HEAD : HALF].unsqueeze(1).to_broadcast([P, ROUND_TILES[r], HEAD]),
                 op=ADD,
             )
 
@@ -256,8 +273,8 @@ def tile_selfattention_pa_t_kernel(
             )
 
         def rotation_terms(r):
-            shape = [P, ROUND, ROT_HEADS, PAIRS, 2]
-            tiles = slice(r * ROUND, (r + 1) * ROUND)
+            shape = [P, ROUND_TILES[r], ROT_HEADS, PAIRS, 2]
+            tiles = slice(FIRST_TILES[r], FIRST_TILES[r] + ROUND_TILES[r])
             pairs = back_rounds[r][:, :, 0 : ROT_HEADS * ROTATED].rearrange(
                 "p t (h j e) -> p t h j e", h=ROT_HEADS, e=2
             )
@@ -285,16 +302,25 @@ def tile_selfattention_pa_t_kernel(
                 out=k_rows[:, :, 0:ROTATED], in0=even[:, :, Q_HEADS], in1=odd[:, :, Q_HEADS], op=ADD
             )
 
-        def store_block(c):
-            q_rows, k_rows, v_rows = out_blocks[c]
-            tiles = slice(c * BLOCK, (c + 1) * BLOCK)
-            nc.sync.dma_start(out=v_dram[:, tiles, :], in_=v_rows[:])
+        def store(first, count):
+            q_rows, k_rows, v_rows = out_blocks[first // BLOCK]
+            inside = slice(first % BLOCK, first % BLOCK + count)
+            tiles = slice(first, first + count)
+            nc.sync.dma_start(out=v_dram[:, tiles, :], in_=v_rows[:, inside])
             nc.sync.dma_start(
-                out=q_dram[:, tiles, :], in_=q_rows[:].rearrange("p t n d -> p t (n d)")
+                out=q_dram[:, tiles, :], in_=q_rows[:, inside].rearrange("p t n d -> p t (n d)")
             )
-            nc.sync.dma_start(out=k_dram[:, tiles, :], in_=k_rows[:])
+            nc.sync.dma_start(out=k_dram[:, tiles, :], in_=k_rows[:, inside])
+
+        def store_finished(r):
+            first, end = FIRST_TILES[r], FIRST_TILES[r] + ROUND_TILES[r]
+            if end > TILES - BLOCK:
+                store(first, end - first)
+            elif end % BLOCK == 0:
+                store(end - BLOCK, BLOCK)
 
         for n in range(ROUNDS + 3):
+            half = ROUND_TILES[n] // 2 if n < ROUNDS else 0
             if n + LOOKAHEAD < ROUNDS:
                 load_round(n + LOOKAHEAD)
             if n >= 3:
@@ -303,21 +329,23 @@ def tile_selfattention_pa_t_kernel(
                 rotation_terms(n - 3)
                 values(n - 3)
             if n < ROUNDS:
-                turn_tiles(n, (0, 1))
+                turn_tiles(n, range(half))
+            if n == 1:
+                quantise_weights()
             if 1 <= n <= ROUNDS:
                 quantise(n - 1)
-            if n == 0:
-                spread_bias()
             if 2 <= n <= ROUNDS + 1:
                 multiply_by_feature(n - 2)
             if n < ROUNDS:
-                turn_tiles(n, (2, 3))
-            if n == 1:
+                turn_tiles(n, range(half, 2 * half))
+            if n == 0:
+                spread_bias()
+                turn_weights()
+            if n == 2:
                 make_angle_tables()
             if n >= 3:
                 rotate(n - 3)
                 rest_of_k(n - 3)
-                if (n - 2) * ROUND % BLOCK == 0:
-                    store_block((n - 3) * ROUND // BLOCK)
+                store_finished(n - 3)
             if 2 <= n <= ROUNDS + 1:
                 multiply_by_token(n - 2)

from contextlib import ExitStack

import concourse.mybir as mybir
from concourse.masks import make_identity

F32 = mybir.dt.float32
BF16 = mybir.dt.bfloat16
U32 = mybir.dt.uint32
U8 = mybir.dt.uint8
FP8X4 = mybir.dt.float8_e4m3fn_x4
ADD = mybir.AluOpType.add
MULT = mybir.AluOpType.mult
IDENTITY = mybir.ActivationFunctionType.Identity

P = 128
POSITIONS, BATCH, WIDTH = 4096, 2, 1024
HEAD = 64
Q_HEADS = 2
FEATURES = 4 * HEAD
HALF = FEATURES // 2
ROTATED = 32
ROT_HEADS = Q_HEADS + 1
PAIRS = ROTATED // 2

PACK = 4
PASSES = WIDTH // (P * PACK)
HALVES = 2

TILES = POSITIONS * BATCH // P
ROUND = 4
BLOCK = 2 * ROUND
ENDS = [ROUND // 2, ROUND // 2]
ROUND_TILES = ENDS + [ROUND] * (TILES // ROUND - 2) + ENDS
ROUNDS = len(ROUND_TILES)
FIRST_TILES = [sum(ROUND_TILES[:r]) for r in range(ROUNDS)]
LOOKAHEAD = 6

FLOPS = 2 * POSITIONS * BATCH * WIDTH * FEATURES


def turn(nc, banks, tag, identity, rows_words):
    bank = banks.tile([P, PASSES, HALVES, P], F32, tag=tag)
    for g in range(PASSES):
        for u in range(HALVES):
            first = (g * HALVES + u) * P
            nc.tensor.transpose(bank[:, g, u, :], rows_words[:, first : first + P], identity)
    return bank


def tile_selfattention_pa_t_kernel(
    tc, hidden_states, Wqkv, bqkv, rotary_pos_emb, out_0, out_1, out_2
):
    nc = tc.nc
    per_partition = POSITIONS // P
    x_dram = hidden_states.rearrange("(p s) b h -> p (s b) h", s=per_partition)
    q_dram = out_0.rearrange("(p s) b n d -> p (s b) (n d)", s=per_partition)
    k_dram = out_1.rearrange("(p s) b n d -> p (s b) (n d)", s=per_partition)
    v_dram = out_2.rearrange("(p s) b n d -> p (s b) (n d)", s=per_partition)
    rope_dram = rotary_pos_emb.rearrange("(p s) o j c -> p s (o j) c", s=per_partition)

    with ExitStack() as ctx:
        ctx.enter_context(tc.manual_schedule())
        const = ctx.enter_context(tc.tile_pool(name="const", bufs=1))
        x_pool = ctx.enter_context(tc.tile_pool(name="x", bufs=LOOKAHEAD + 1))
        mx_pool = ctx.enter_context(tc.tile_pool(name="mx", bufs=3))
        out_pool = ctx.enter_context(tc.tile_pool(name="out", bufs=3))
        scratch = ctx.enter_context(tc.tile_pool(name="scratch", bufs=2))
        turned_banks = ctx.enter_context(tc.psum_pool(name="turned", bufs=3))
        fm_banks = ctx.enter_context(tc.psum_pool(name="by_feature", bufs=1))
        back_banks = ctx.enter_context(tc.psum_pool(name="back", bufs=2))
        tm_banks = ctx.enter_context(tc.psum_pool(name="by_token", bufs=2))

        x_rounds = {}

        def load_round(r):
            count, first = ROUND_TILES[r], FIRST_TILES[r]
            x_rows = x_pool.tile([P, count, WIDTH], BF16)
            piece = 1 if r == 0 else 2 if r <= 3 else count
            for t in range(0, count, piece):
                nc.sync.dma_start(
                    out=x_rows[:, t : t + piece], in_=x_dram[:, first + t : first + t + piece, :]
                )
            x_rounds[r] = x_rows

        rope_rows = const.tile([P, per_partition, PAIRS, 2], BF16)
        bias_in = const.tile([P, FEATURES], BF16)
        w_rows = const.tile([P, FEATURES // P, WIDTH], BF16)
        nc.sync.dma_start(out=bias_in[0:1, :], in_=bqkv.rearrange("(o f) -> o f", o=1))
        load_round(0)
        nc.sync.dma_start(out=w_rows[:], in_=Wqkv.rearrange("(i p) k -> p i k", p=P))
        load_round(1)
        nc.sync.dma_start(out=rope_rows[:], in_=rope_dram)
        for r in range(2, LOOKAHEAD):
            load_round(r)

        identity = const.tile([P, P], F32)
        make_identity(nc, identity[:])
        ones = const.tile([P, P], BF16)
        nc.vector.memset(ones[:], 1.0)

        def in_order(columns):
            parts = columns.rearrange("p (s c) w -> p s c w", s=2)
            q = parts[:, :, 0 : Q_HEADS * ROTATED].rearrange("p s (n r) w -> p n s r w", r=ROTATED)
            return q, parts[:, :, Q_HEADS * ROTATED : HALF]

        bias_row = const.tile([P, FEATURES, 1], BF16)
        nc.vector.memset(bias_row[:], 0.0)
        bias_tm = const.tile([P, HALF], F32)
        bias_fm = const.tile([P, 1], F32)

        def spread_bias():
            q, kv = in_order(bias_row[0:1])
            nc.vector.tensor_copy(
                out=q, in_=bias_in[0:1, 0:HALF].rearrange("p (n s r w) -> p n s r w", n=Q_HEADS, s=2, w=1)
            )
            nc.vector.tensor_copy(
                out=kv, in_=bias_in[0:1, HALF:FEATURES].rearrange("p (s c w) -> p s c w", s=2, w=1)
            )
            row = bias_row[:].rearrange("p f w -> p (f w)")
            bank = back_banks.tile([P, HALF + 1], F32, tag="back")
            nc.tensor.matmul(bank[:, 0:HALF], lhsT=ones[:], rhs=row[:, HALF:FEATURES], start=True, stop=True)
            nc.tensor.matmul(bank[:, HALF : HALF + 1], lhsT=row[:, 0:HALF], rhs=ones[:, 0:1], start=True, stop=True)
            nc.scalar.copy(out=bias_tm[:], in_=bank[:, 0:HALF])
            nc.scalar.copy(out=bias_fm[:], in_=bank[:, HALF : HALF + 1])

        cos_sin = const.tile([P, TILES, PAIRS, 2], BF16)
        minus_sin_cos = const.tile([P, TILES, PAIRS, 2], BF16)

        def make_angle_tables():
            def by_position(table):
                return table.rearrange("p (i b) j e -> p i b j e", b=BATCH)

            shape = [P, per_partition, BATCH, PAIRS]
            sin = rope_rows[:, :, :, 1].unsqueeze(2).to_broadcast(shape)
            cos = rope_rows[:, :, :, 0].unsqueeze(2).to_broadcast(shape)
            nc.vector.tensor_copy(
                out=cos_sin[:].rearrange("p (i b) j e -> p i b (j e)", b=BATCH),
                in_=rope_rows[:]
                .rearrange("p i j e -> p i (j e)")
                .unsqueeze(2)
                .to_broadcast([P, per_partition, BATCH, 2 * PAIRS]),
            )
            nc.vector.tensor_scalar_mul(
                out=by_position(minus_sin_cos[:])[:, :, :, :, 0], in0=sin, scalar1=-1.0
            )
            nc.vector.tensor_copy(out=by_position(minus_sin_cos[:])[:, :, :, :, 1], in_=cos)

        w_grouped = const.tile([P, PASSES, FEATURES, PACK], BF16, align_bytes=64)
        w_codes = const.tile([P, PASSES, FEATURES], U32, align_bytes=64)
        w_scales = const.tile([P, PASSES, FEATURES], U8, align_bytes=64)

        def turn_weights():
            for i in range(FEATURES // P):
                bank = turn(nc, tm_banks, "by_token", identity[:], w_rows[:, i, :].bitcast(F32))
                for g in range(PASSES):
                    words = bank[:, g].rearrange("p u f -> p f u")
                    q, kv = in_order(w_grouped[:].bitcast(F32)[:, g])
                    if i == 0:
                        nc.vector.tensor_copy(
                            out=q, in_=words.rearrange("p (n s r) u -> p n s r u", n=Q_HEADS, s=2)
                        )
                    else:
                        nc.vector.tensor_copy(
                            out=kv, in_=words.rearrange("p (s c) u -> p s c u", s=2)
                        )

        def quantise_weights():
            nc.vector.quantize_mx(
                out=w_codes[:].rearrange("p g n -> p (g n)").bitcast(FP8X4),
                scales=w_scales[:].rearrange("p g n -> p (g n)"),
                in_=w_grouped[:].rearrange("p g n k -> p (g n k)"),
            )

        grouped_rounds, codes_rounds, fm_rounds, tm_rounds = {}, {}, {}, {}
        back_rounds, term_rounds, out_blocks = {}, {}, {}

        def turn_tiles(r, tiles):
            if r not in grouped_rounds:
                x_grouped = mx_pool.tile([P, PASSES, ROUND_TILES[r], P, PACK], BF16, align_bytes=64)
                grouped_rounds[r] = x_grouped
            for t in tiles:
                bank = turn(nc, turned_banks, "turned", identity[:], x_rounds[r][:, t, :].bitcast(F32))
                nc.scalar.copy(
                    out=grouped_rounds[r][:].bitcast(F32)[:, :, t],
                    in_=bank[:].rearrange("p g u r -> p g r u"),
                )

        def quantise(r):
            x_codes = mx_pool.tile([P, PASSES, ROUND_TILES[r] * P], U32, align_bytes=64)
            x_scales = mx_pool.tile([P, PASSES, ROUND_TILES[r] * P], U8, align_bytes=64)
            nc.vector.quantize_mx(
                out=x_codes[:].rearrange("p g n -> p (g n)").bitcast(FP8X4),
                scales=x_scales[:].rearrange("p g n -> p (g n)"),
                in_=grouped_rounds[r][:].rearrange("p g t n k -> p (g t n k)"),
            )
            codes_rounds[r] = (x_codes, x_scales)

        def multiply_by_feature(r):
            x_codes, x_scales = codes_rounds[r]
            bank = fm_banks.tile([P, ROUND_TILES[r] * P], F32)
            for g in range(PASSES):
                nc.tensor.matmul_mx(
                    out=bank[:],
                    lhsT=w_codes[:, g, 0:HALF].bitcast(FP8X4),
                    lhsT_scale=w_scales[:, g, 0:HALF],
                    rhs=x_codes[:, g, :].bitcast(FP8X4),
                    rhs_scale=x_scales[:, g, :],
                    start=(g == 0),
                    stop=(g == PASSES - 1),
                )
            fm_rows = scratch.tile([P, ROUND_TILES[r] * P], F32)
            nc.scalar.activation(out=fm_rows[:], in_=bank[:], func=IDENTITY, bias=bias_fm[:, 0:1])
            fm_rounds[r] = fm_rows

        def multiply_by_token(r):
            x_codes, x_scales = codes_rounds[r]
            bank = tm_banks.tile([P, ROUND_TILES[r], HALF], F32, tag="by_token")
            for t in range(ROUND_TILES[r]):
                for g in range(PASSES):
                    nc.tensor.matmul_mx(
                        out=bank[:, t, :],
                        lhsT=x_codes[:, g, t * P : (t + 1) * P].bitcast(FP8X4),
                        lhsT_scale=x_scales[:, g, t * P : (t + 1) * P],
                        rhs=w_codes[:, g, HALF:FEATURES].bitcast(FP8X4),
                        rhs_scale=w_scales[:, g, HALF:FEATURES],
                        start=(g == 0),
                        stop=(g == PASSES - 1),
                    )
            tm_rounds[r] = bank

        def turn_back(r):
            bank = back_banks.tile([P, ROUND_TILES[r], HALF], F32, tag="back")
            for t in range(ROUND_TILES[r]):
                nc.tensor.transpose(bank[:, t, :], fm_rounds[r][:, t * P : (t + 1) * P], identity[:])
            back_rounds[r] = bank

        def rows_of(r):
            block, first = divmod(FIRST_TILES[r], BLOCK)
            if block not in out_blocks:
                q_rows = out_pool.tile([P, BLOCK, Q_HEADS, HEAD], F32)
                k_rows = out_pool.tile([P, BLOCK, HEAD], F32)
                v_rows = out_pool.tile([P, BLOCK, HEAD], F32)
                out_blocks[block] = (q_rows, k_rows, v_rows)
            q_rows, k_rows, v_rows = out_blocks[block]
            tiles = slice(first, first + ROUND_TILES[r])
            return q_rows[:, tiles], k_rows[:, tiles], v_rows[:, tiles]

        def rest_of_q(r):
            shape = [P, ROUND_TILES[r], Q_HEADS, HEAD - ROTATED]
            first_v = Q_HEADS * (HEAD - ROTATED)
            nc.vector.tensor_tensor(
                out=rows_of(r)[0][:, :, :, ROTATED:HEAD],
                in0=tm_rounds[r][:, :, 0:first_v].rearrange("p t (n d) -> p t n d", n=Q_HEADS),
                in1=bias_tm[:, 0:first_v]
                .rearrange("p (n d) -> p n d", n=Q_HEADS)
                .unsqueeze(1)
                .to_broadcast(shape),
                op=ADD,
            )

        def values(r):
            nc.vector.tensor_tensor(
                out=rows_of(r)[2],
                in0=tm_rounds[r][:, :, HALF - HEAD : HALF],
                in1=bias_tm[:, HALF - HEAD : HALF].unsqueeze(1).to_broadcast([P, ROUND_TILES[r], HEAD]),
                op=ADD,
            )

        def rest_of_k(r):
            nc.scalar.copy(
                out=rows_of(r)[1][:, :, ROTATED:HEAD],
                in_=back_rounds[r][:, :, ROT_HEADS * ROTATED : HALF],
            )

        def rotation_terms(r):
            shape = [P, ROUND_TILES[r], ROT_HEADS, PAIRS, 2]
            tiles = slice(FIRST_TILES[r], FIRST_TILES[r] + ROUND_TILES[r])
            pairs = back_rounds[r][:, :, 0 : ROT_HEADS * ROTATED].rearrange(
                "p t (h j e) -> p t h j e", h=ROT_HEADS, e=2
            )
            from_even = scratch.tile(shape, F32)
            from_odd = scratch.tile(shape, F32)
            for term, e, table in ((from_even, 0, cos_sin), (from_odd, 1, minus_sin_cos)):
                nc.vector.tensor_tensor(
                    out=term[:],
                    in0=pairs[:, :, :, :, e : e + 1].to_broadcast(shape),
                    in1=table[:, tiles].unsqueeze(2).to_broadcast(shape),
                    op=MULT,
                )
            term_rounds[r] = (from_even, from_odd)

        def rotate(r):
            q_rows, k_rows, v_rows = rows_of(r)
            even, odd = [t[:].rearrange("p t h j e -> p t h (j e)") for t in term_rounds[r]]
            nc.vector.tensor_tensor(
                out=q_rows[:, :, :, 0:ROTATED],
                in0=even[:, :, 0:Q_HEADS],
                in1=odd[:, :, 0:Q_HEADS],
                op=ADD,
            )
            nc.vector.tensor_tensor(
                out=k_rows[:, :, 0:ROTATED], in0=even[:, :, Q_HEADS], in1=odd[:, :, Q_HEADS], op=ADD
            )

        def store(first, count):
            q_rows, k_rows, v_rows = out_blocks[first // BLOCK]
            inside = slice(first % BLOCK, first % BLOCK + count)
            tiles = slice(first, first + count)
            nc.sync.dma_start(out=v_dram[:, tiles, :], in_=v_rows[:, inside])
            nc.sync.dma_start(
                out=q_dram[:, tiles, :], in_=q_rows[:, inside].rearrange("p t n d -> p t (n d)")
            )
            nc.sync.dma_start(out=k_dram[:, tiles, :], in_=k_rows[:, inside])

        def store_finished(r):
            first, end = FIRST_TILES[r], FIRST_TILES[r] + ROUND_TILES[r]
            if end > TILES - BLOCK:
                store(first, end - first)
            elif end % BLOCK == 0:
                store(end - BLOCK, BLOCK)

        for n in range(ROUNDS + 3):
            half = ROUND_TILES[n] // 2 if n < ROUNDS else 0
            if n + LOOKAHEAD < ROUNDS:
                load_round(n + LOOKAHEAD)
            if n >= 3:
                turn_back(n - 3)
                rest_of_q(n - 3)
                rotation_terms(n - 3)
                values(n - 3)
            if n < ROUNDS:
                turn_tiles(n, range(half))
            if n == 1:
                quantise_weights()
            if 1 <= n <= ROUNDS:
                quantise(n - 1)
            if 2 <= n <= ROUNDS + 1:
                multiply_by_feature(n - 2)
            if n < ROUNDS:
                turn_tiles(n, range(half, 2 * half))
            if n == 0:
                spread_bias()
                turn_weights()
            if n == 2:
                make_angle_tables()
            if n >= 3:
                rotate(n - 3)
                rest_of_k(n - 3)
                store_finished(n - 3)
            if 2 <= n <= ROUNDS + 1:
                multiply_by_token(n - 2)
